import numpy as np
import ml_dtypes


def mxq(x, axis, fmt="e4m3"):
    dtype, down = {"e4m3": (ml_dtypes.float8_e4m3fn, 7), "e5m2": (ml_dtypes.float8_e5m2, 14)}[fmt]
    v = np.moveaxis(np.asarray(x, np.float32).astype(ml_dtypes.bfloat16).astype(np.float64), axis, -1)
    blocks = v.reshape(v.shape[:-1] + (-1, 32))
    amax = np.abs(blocks).max(-1, keepdims=True)
    byte = np.maximum(np.where(amax > 0, np.frexp(amax)[1] - 1 + 127, 0) - down, 1)
    scale = np.exp2(byte - 127.0)
    codes = (blocks / scale).astype(np.float32).astype(dtype).astype(np.float64)
    return np.moveaxis((codes * scale).reshape(v.shape), -1, axis)


WIDE = False


def mx_kscale(k):
    if not WIDE:
        return np.ones(k)
    levels = np.array([10, -10, 5, -5, 0])
    a = np.random.permutation(np.resize(levels, k // 512 * 4)).reshape(k // 512, 4)
    idx = np.arange(k)
    return np.exp2(a[idx // 512, idx % 128 // 32])


BF16 = ml_dtypes.bfloat16


def bf(x):
    return np.asarray(x, np.float32).astype(BF16)


def f64(x):
    return np.asarray(x).astype(np.float64)


E2M1 = np.array([0.0, 0.5, 1.0, 1.5, 2.0, 3.0, 4.0, 6.0, -0.0, -0.5, -1.0, -1.5, -2.0, -3.0, -4.0, -6.0])


def pack_weight(w, fmt):
    k, n = w.shape
    w = f64(bf(w)).reshape(k // 32, 32, n)
    amax = np.abs(w).max(1)
    if fmt == "e4m3":
        byte = np.frexp(amax)[1] - 1 + 127 - 7
    else:
        mant, ex = np.frexp(amax / 6.0)
        byte = np.where(mant > 0.5, ex, ex - 1) + 127
    byte = np.clip(np.where(amax > 0, byte, 1), 1, 254)
    scaled = (w * np.exp2(127.0 - byte)[:, None, :]).reshape(k, n).astype(np.float32)
    by_word = np.ascontiguousarray(scaled.reshape(k // 512, 128, 4, n).transpose(0, 1, 3, 2))
    if fmt == "e4m3":
        words = by_word.astype(ml_dtypes.float8_e4m3fn).view(np.uint8)
    else:
        c = by_word.astype(ml_dtypes.float4_e2m1fn).view(np.uint8) & 0xF
        words = c[..., 0::2] | (c[..., 1::2] << 4)
    return np.ascontiguousarray(words), np.ascontiguousarray(byte.astype(np.uint8).reshape(k // 512, 16, n))


def unpack_weight(words, scales, fmt):
    g, p, n, _ = words.shape
    if fmt == "e4m3":
        vals = np.ascontiguousarray(words).view(ml_dtypes.float8_e4m3fn).astype(np.float64)
    else:
        nib = np.empty((g, p, n, 4), np.uint8)
        nib[..., 0::2] = words & 0xF
        nib[..., 1::2] = words >> 4
        vals = E2M1[nib]
    vals = vals * np.repeat(np.exp2(scales.astype(np.float64) - 127.0), 8, axis=1)[..., None]
    return vals.transpose(0, 1, 3, 2).reshape(g * 512, n)


N, D_IN, H0, H1, K = 8192, 512, 512, 256, 20
V = 1.0
FMT = "e4m3"


def silu(v):
    return v / (1.0 + np.exp(-v))


def setup_inputs():
    s = mx_kscale(D_IN)
    w1 = np.random.standard_normal((D_IN, H0)) / np.sqrt(D_IN)
    b1 = np.random.standard_normal(H0) * 0.2
    w2 = np.random.standard_normal((H0, H1)) * 4.0 / np.sqrt(H0 * H1)
    b2 = np.random.standard_normal(H1) * 0.1
    cent = np.random.standard_normal((K, D_IN)) * 0.9
    x = cent[np.random.randint(0, K, N)] + np.random.standard_normal((N, D_IN)) * 0.44
    hc = silu(np.stack([(c[:, None] * w1).sum(0) for c in cent]) + b1)
    clusters = (hc[:, :, None] * w2[None]).sum(1) + b2 + np.random.standard_normal((K, H1)) * 0.5 / np.sqrt(H1)
    W1_words, W1_scales = pack_weight(w1 / s[:, None], FMT)
    W2_words, W2_scales = pack_weight(w2, FMT)
    return {"x": bf(x * s), "W1_words": W1_words, "W1_scales": W1_scales, "b1": bf(b1), "W2_words": W2_words, "W2_scales": W2_scales, "b2": bf(b2), "clusters": bf(clusters)}


def reference(x, W1_words, W1_scales, b1, W2_words, W2_scales, b2, clusters):
    h = silu((mxq(f64(x), 1, "e4m3") @ unpack_weight(W1_words, W1_scales, FMT)) + f64(b1))
    z = (mxq(h, 1, "e4m3") @ unpack_weight(W2_words, W2_scales, FMT)) + f64(b2)
    d2 = np.stack([((z - c) ** 2).sum(1) for c in f64(clusters)], axis=1)
    q = 1.0 / (1.0 + d2 / V)
    q = q ** ((V + 1.0) / 2.0)
    q = q / q.sum(1, keepdims=True)
    return z, q

@@ -1,0 +1,297 @@
+from contextlib import ExitStack
+
+import concourse.mybir as mybir
+from concourse.masks import make_identity
+
+F32 = mybir.dt.float32
+BF16 = mybir.dt.bfloat16
+I32 = mybir.dt.int32
+U32 = mybir.dt.uint32
+U8 = mybir.dt.uint8
+FP8X4 = mybir.dt.float8_e4m3fn_x4
+ACT = mybir.ActivationFunctionType
+ALU = mybir.AluOpType
+AXIS = mybir.AxisListType
+
+P = 128
+PACK = 4
+ROWS, D_IN, H0, H1, K = 8192, 512, 512, 256, 20
+TILES = ROWS // P
+GROUP = 4
+GROUPS = TILES // GROUP
+COLS = GROUP * P
+AHEAD = 4
+BATCH = 2
+
+FLOPS = 2 * ROWS * (D_IN * H0 + H0 * H1 + H1 * K)
+
+
+def tile_lintrans_pa_t_kernel(
+    tc, x, W1_words, W1_scales, b1, W2_words, W2_scales, b2, clusters, out_0, out_1
+):
+    nc = tc.nc
+    x_rows = x.rearrange("(p t) k -> p t k", t=TILES)
+    z_rows = out_0.rearrange("(p t) j -> p t j", t=TILES)
+    q_rows = out_1.rearrange("(p t) k -> p t k", t=TILES)
+
+    with ExitStack() as ctx:
+        consts = ctx.enter_context(tc.tile_pool(name="consts", bufs=1))
+        x_pool = ctx.enter_context(tc.tile_pool(name="x_pool", bufs=AHEAD + 2))
+        work = ctx.enter_context(tc.tile_pool(name="work", bufs=3))
+        banks = ctx.enter_context(tc.psum_pool(name="banks", bufs=7))
+        dist_bank = ctx.enter_context(tc.psum_pool(name="dist_bank", bufs=1))
+        ctx.enter_context(tc.manual_schedule())
+
+        x_tiles, x_grouped, x_quantised = {}, {}, {}
+        h_rows, h_grouped, h_quantised = {}, {}, {}
+        z_tiles, z_transposed, dist_tiles = {}, {}, {}
+
+        def load_x(g):
+            x_sb = x_pool.tile([P, GROUP, D_IN], BF16)
+            nc.sync.dma_start(out=x_sb[:], in_=x_rows[:, g * GROUP : (g + 1) * GROUP, :])
+            x_tiles[g] = x_sb
+
+        w1s_raw = consts.tile([P, H0], U8, align_bytes=64)
+        w2s = consts.tile([P, H1], U8, align_bytes=64)
+        small = consts.tile([P, 3, P], BF16)
+        nc.vector.memset(small[:], 0.0)
+        nc.vector.memset(w1s_raw[:].bitcast(I32), 0)
+        nc.vector.memset(w2s[:].bitcast(I32), 0)
+
+        nc.sync.dma_start(out=small[0:PACK, 0, :], in_=b1.rearrange("(a s i) -> s a i", s=PACK, i=PACK))
+        nc.sync.dma_start(out=small[0:K, 1:3, :], in_=clusters.rearrange("k (h j) -> k h j", h=2))
+        nc.sync.dma_start(out=small[K : K + 1, 1:3, :], in_=b2.rearrange("(o h j) -> o h j", o=1, h=2))
+        b2_bf = consts.tile([P, H1], BF16)
+        nc.sync.dma_start(out=b2_bf[:], in_=b2.partition_broadcast(P))
+        load_x(0)
+        w1_raw = consts.tile([P, H0], U32, align_bytes=64)
+        nc.sync.dma_start(
+            out=w1_raw[:].bitcast(I32),
+            in_=W1_words[0].rearrange("p n t -> p (n t)").bitcast(I32),
+        )
+        for quad in range(4):
+            nc.sync.dma_start(
+                out=w1s_raw[32 * quad : 32 * quad + 4, :].bitcast(I32),
+                in_=W1_scales[0, 4 * quad : 4 * quad + 4, :].bitcast(I32),
+            )
+        load_x(1)
+        w2c = consts.tile([P, H1], U32, align_bytes=64)
+        nc.sync.dma_start(
+            out=w2c[:].bitcast(I32),
+            in_=W2_words[0].rearrange("p n t -> p (n t)").bitcast(I32),
+        )
+        for quad in range(4):
+            nc.sync.dma_start(
+                out=w2s[32 * quad : 32 * quad + 4, :].bitcast(I32),
+                in_=W2_scales[0, 4 * quad : 4 * quad + 4, :].bitcast(I32),
+            )
+        for g in range(2, AHEAD):
+            load_x(g)
+
+        ident = consts.tile([P, P], F32)
+        make_identity(nc, ident[:])
+        ones = consts.tile([P, P], F32)
+        nc.vector.memset(ones[:], 1.0)
+        small_f = consts.tile([P, 3, P], F32)
+        nc.vector.tensor_copy(out=small_f[:], in_=small[:])
+        small_ps = banks.tile([P, 3, P], F32, tag="bank")
+        for b in range(3):
+            nc.tensor.transpose(out=small_ps[:, b, :], in_=small_f[:, b, :], identity=ident[:])
+        small_t = consts.tile([P, 3, P], F32)
+        nc.vector.tensor_copy(out=small_t[:], in_=small_ps[:])
+        b1_cols = small_t[:, 0, 0:PACK]
+        c_t = small_t[:, 1:3, 0:K]
+        b2_cols = small_t[:, 1:3, K]
+        c_minus2 = consts.tile([P, 2, K], F32)
+        nc.vector.tensor_scalar_mul(out=c_minus2[:], in0=c_t, scalar1=-2.0)
+        c_sq = consts.tile([P, 2, K], F32)
+        nc.vector.tensor_tensor(out=c_sq[:], in0=c_t, in1=c_t, op=ALU.mult)
+        c_norm_ps = banks.tile([P, K], F32, tag="bank")
+        for half in range(2):
+            nc.tensor.matmul(
+                out=c_norm_ps[:], lhsT=ones[:], rhs=c_sq[:, half, :], start=(half == 0), stop=(half == 1)
+            )
+        c_norm1 = consts.tile([P, K], F32)
+        nc.vector.tensor_scalar_add(out=c_norm1[:], in0=c_norm_ps[:], scalar1=1.0)
+        b2_bc = consts.tile([P, H1], F32)
+        nc.vector.tensor_copy(out=b2_bc[:], in_=b2_bf[:])
+
+        w1c = consts.tile([P, PACK, P], U32, align_bytes=64)
+        nc.vector.tensor_copy(
+            out=w1c[:].bitcast(I32).rearrange("p s (a i) -> p s a i", i=PACK),
+            in_=w1_raw[:].bitcast(I32).rearrange("p (a s i) -> p s a i", s=PACK, i=PACK),
+        )
+        w1s = consts.tile([P, PACK, P], U8, align_bytes=64)
+        nc.vector.tensor_copy(
+            out=w1s[:].bitcast(I32),
+            in_=w1s_raw[:].bitcast(I32).rearrange("p (a s) -> p s a", s=PACK),
+        )
+
+        z_norm = consts.tile([P, TILES], F32)
+        q_sb = consts.tile([P, TILES, K], F32)
+
+        def transpose_x(g):
+            grouped = work.tile([P, PACK * COLS], BF16, align_bytes=64, name="x_grouped")
+            grouped_words = grouped[:].bitcast(F32).rearrange("p (i r u) -> p i r u", i=GROUP, u=2)
+            for pair in range(2):
+                x_t = banks.tile([P, 2, 2, P], F32, tag="bank")
+                for i in range(2):
+                    words = x_tiles[g][:, 2 * pair + i, :].bitcast(F32)
+                    for u in range(2):
+                        nc.tensor.transpose(out=x_t[:, i, u, :], in_=words[:, u : D_IN // 2 : 2], identity=ident[:])
+                nc.scalar.copy(
+                    out=grouped_words[:, 2 * pair : 2 * pair + 2], in_=x_t[:].rearrange("p i u r -> p i r u")
+                )
+            x_grouped[g] = grouped
+
+        def quantise_x(g):
+            codes = work.tile([P, COLS], U32, align_bytes=64, name="x_codes")
+            scales = work.tile([P, COLS], U8, align_bytes=64, name="x_scales")
+            nc.vector.quantize_mx(out=codes[:].bitcast(FP8X4), scales=scales[:], in_=x_grouped[g][:])
+            x_quantised[g] = (codes, scales)
+
+        def first_matmul(g):
+            codes, scales = x_quantised[g]
+            h_t = work.tile([P, PACK, COLS], BF16)
+            rows = work.tile([P, PACK, COLS], BF16, name="h_rows")
+            for s in range(PACK):
+                h_ps = banks.tile([P, COLS], F32, tag="bank")
+                nc.tensor.matmul_mx(
+                    out=h_ps[:],
+                    lhsT=w1c[:, s, :].bitcast(FP8X4),
+                    lhsT_scale=w1s[:, s, :],
+                    rhs=codes[:].bitcast(FP8X4),
+                    rhs_scale=scales[:],
+                    start=True,
+                    stop=True,
+                )
+                nc.scalar.activation(
+                    out=h_t[:, s, :], in_=h_ps[:], func=ACT.Silu, bias=b1_cols[:, s : s + 1], scale=1.0
+                )
+                nc.sync.dma_start(out=rows[s:P:PACK, :, :], in_=h_t[:, s, :])
+            h_rows[g] = rows
+
+        def regroup_h(g):
+            grouped = work.tile([P, COLS, PACK], BF16, align_bytes=64, name="h_grouped")
+            nc.vector.tensor_copy(
+                out=grouped[:].rearrange("p (c i) t -> p c t i", i=4),
+                in_=h_rows[g][:].rearrange("p t (c i) -> p c t i", i=4),
+            )
+            h_grouped[g] = grouped
+
+        def quantise_h(g):
+            codes = work.tile([P, COLS], U32, align_bytes=64, name="h_codes")
+            scales = work.tile([P, COLS], U8, align_bytes=64, name="h_scales")
+            nc.vector.quantize_mx(
+                out=codes[:].bitcast(FP8X4), scales=scales[:], in_=h_grouped[g][:].rearrange("p c t -> p (c t)")
+            )
+            h_quantised[g] = (codes, scales)
+
+        def second_matmul(g):
+            codes, scales = h_quantised[g]
+            z_sb = work.tile([P, GROUP, H1], F32)
+            for pair in range(2):
+                z_ps = banks.tile([P, 2, H1], F32, tag="bank")
+                for i in range(2):
+                    cols = slice((2 * pair + i) * P, (2 * pair + i + 1) * P)
+                    nc.tensor.matmul_mx(
+                        out=z_ps[:, i, :],
+                        lhsT=codes[:, cols].bitcast(FP8X4),
+                        lhsT_scale=scales[:, cols],
+                        rhs=w2c[:].bitcast(FP8X4),
+                        rhs_scale=w2s[:],
+                        start=True,
+                        stop=True,
+                    )
+                nc.vector.tensor_tensor(
+                    out=z_sb[:, 2 * pair : 2 * pair + 2, :],
+                    in0=z_ps[:],
+                    in1=b2_bc[:].unsqueeze(1).to_broadcast([P, 2, H1]),
+                    op=ALU.add,
+                )
+            nc.sync.dma_start(out=z_rows[:, g * GROUP : (g + 1) * GROUP, :], in_=z_sb[:])
+            z_tiles[g] = z_sb
+            z_t = work.tile([P, 2, COLS], F32)
+            for half in range(2):
+                z_t_ps = banks.tile([P, COLS], F32, tag="bank")
+                nc.tensor.matmul_mx(
+                    out=z_t_ps[:],
+                    lhsT=w2c[:, half * P : (half + 1) * P].bitcast(FP8X4),
+                    lhsT_scale=w2s[:, half * P : (half + 1) * P],
+                    rhs=codes[:].bitcast(FP8X4),
+                    rhs_scale=scales[:],
+                    start=True,
+                    stop=True,
+                )
+                if half == 0:
+                    nc.vector.tensor_scalar_add(out=z_t[:, half, :], in0=z_t_ps[:], scalar1=b2_cols[:, half : half + 1])
+                else:
+                    nc.scalar.activation(
+                        out=z_t[:, half, :], in_=z_t_ps[:], func=ACT.Identity, bias=b2_cols[:, half : half + 1], scale=1.0
+                    )
+            z_transposed[g] = z_t
+
+        def distances(g):
+            for i in range(GROUP):
+                t = g * GROUP + i
+                squares = work.tile([P, H1], BF16)
+                nc.scalar.activation(
+                    out=squares[:], in_=z_tiles[g][:, i, :], func=ACT.Square, accum_out=z_norm[:, t : t + 1]
+                )
+            if g % BATCH == 0:
+                dist_ps = dist_bank.tile([P, BATCH * GROUP, K], F32)
+                dist_tiles[g // BATCH] = dist_ps
+            for i in range(GROUP):
+                for half in range(2):
+                    nc.tensor.matmul(
+                        out=dist_tiles[g // BATCH][:, (g % BATCH) * GROUP + i, :],
+                        lhsT=z_transposed[g][:, half, i * P : (i + 1) * P],
+                        rhs=c_minus2[:, half, :],
+                        start=(half == 0),
+                        stop=(half == 1),
+                    )
+
+        def assign(batch):
+            n = BATCH * GROUP
+            tiles = slice(batch * n, (batch + 1) * n)
+            shape = [P, n, K]
+            denom = work.tile(shape, F32)
+            nc.vector.tensor_tensor(
+                out=denom[:], in0=dist_tiles[batch][:], in1=c_norm1[:].unsqueeze(1).to_broadcast(shape), op=ALU.add
+            )
+            nc.vector.tensor_tensor(
+                out=denom[:], in0=denom[:], in1=z_norm[:, tiles].unsqueeze(2).to_broadcast(shape), op=ALU.add
+            )
+            kernel = work.tile(shape, F32)
+            nc.vector.reciprocal(out=kernel[:], in_=denom[:])
+            total = work.tile([P, n], F32)
+            nc.vector.tensor_reduce(out=total[:], in_=kernel[:], axis=AXIS.X, op=ALU.add)
+            inverse = work.tile([P, n], F32)
+            nc.vector.reciprocal(out=inverse[:], in_=total[:])
+            nc.vector.tensor_tensor(
+                out=q_sb[:, tiles, :], in0=kernel[:], in1=inverse[:].unsqueeze(2).to_broadcast(shape), op=ALU.mult
+            )
+            nc.sync.dma_start(out=q_rows[:, tiles, :], in_=q_sb[:, tiles, :])
+
+        def is_group(g):
+            return 0 <= g < GROUPS
+
+        for n in range(GROUPS + 4):
+            if is_group(n + AHEAD):
+                load_x(n + AHEAD)
+            if is_group(n):
+                transpose_x(n)
+            if is_group(n - 2):
+                regroup_h(n - 2)
+            if is_group(n):
+                quantise_x(n)
+            if is_group(n - 2):
+                quantise_h(n - 2)
+            if is_group(n - 3):
+                second_matmul(n - 3)
+            if is_group(n - 4):
+                distances(n - 4)
+            if is_group(n):
+                first_matmul(n)
+            if is_group(n - 4) and (n - 4) % BATCH == BATCH - 1:
+                assign((n - 4) // BATCH)

@@ -276,22 +276,22 @@ def tile_lintrans_pa_t_kernel(
         def is_group(g):
             return 0 <= g < GROUPS
 
-        for n in range(GROUPS + 4):
+        for n in range(GROUPS + 6):
             if is_group(n + AHEAD):
                 load_x(n + AHEAD)
             if is_group(n):
                 transpose_x(n)
-            if is_group(n - 2):
-                regroup_h(n - 2)
+            if is_group(n - 3):
+                regroup_h(n - 3)
+            if is_group(n - 6) and (n - 6) % BATCH == BATCH - 1:
+                assign((n - 6) // BATCH)
             if is_group(n):
                 quantise_x(n)
-            if is_group(n - 2):
-                quantise_h(n - 2)
+            if is_group(n - 1):
+                first_matmul(n - 1)
             if is_group(n - 3):
-                second_matmul(n - 3)
+                quantise_h(n - 3)
             if is_group(n - 4):
-                distances(n - 4)
-            if is_group(n):
-                first_matmul(n)
-            if is_group(n - 4) and (n - 4) % BATCH == BATCH - 1:
-                assign((n - 4) // BATCH)
+                second_matmul(n - 4)
+            if is_group(n - 5):
+                distances(n - 5)

@@ -53,14 +53,15 @@ def tile_lintrans_pa_t_kernel(
 
         w1s_raw = consts.tile([P, H0], U8, align_bytes=64)
         w2s = consts.tile([P, H1], U8, align_bytes=64)
-        small = consts.tile([P, 3, P], BF16)
+        small = consts.tile([P, 2, P], BF16)
         nc.vector.memset(small[:], 0.0)
         nc.vector.memset(w1s_raw[:].bitcast(I32), 0)
         nc.vector.memset(w2s[:].bitcast(I32), 0)
 
-        nc.sync.dma_start(out=small[0:PACK, 0, :], in_=b1.rearrange("(a s i) -> s a i", s=PACK, i=PACK))
-        nc.sync.dma_start(out=small[0:K, 1:3, :], in_=clusters.rearrange("k (h j) -> k h j", h=2))
-        nc.sync.dma_start(out=small[K : K + 1, 1:3, :], in_=b2.rearrange("(o h j) -> o h j", o=1, h=2))
+        b1_bf = consts.tile([P, PACK], BF16)
+        nc.sync.dma_start(out=b1_bf[:], in_=b1.rearrange("(m t) -> m t", t=PACK))
+        nc.sync.dma_start(out=small[0:K, :, :], in_=clusters.rearrange("k (h j) -> k h j", h=2))
+        nc.sync.dma_start(out=small[K : K + 1, :, :], in_=b2.rearrange("(o h j) -> o h j", o=1, h=2))
         b2_bf = consts.tile([P, H1], BF16)
         nc.sync.dma_start(out=b2_bf[:], in_=b2.partition_broadcast(P))
         load_x(0)
@@ -92,16 +93,17 @@ def tile_lintrans_pa_t_kernel(
         make_identity(nc, ident[:])
         ones = consts.tile([P, P], F32)
         nc.vector.memset(ones[:], 1.0)
-        small_f = consts.tile([P, 3, P], F32)
+        b1_cols = consts.tile([P, PACK], F32)
+        nc.vector.tensor_copy(out=b1_cols[:], in_=b1_bf[:])
+        small_f = consts.tile([P, 2, P], F32)
         nc.vector.tensor_copy(out=small_f[:], in_=small[:])
-        small_ps = banks.tile([P, 3, P], F32, tag="bank")
-        for b in range(3):
-            nc.tensor.transpose(out=small_ps[:, b, :], in_=small_f[:, b, :], identity=ident[:])
-        small_t = consts.tile([P, 3, P], F32)
+        small_ps = banks.tile([P, 2, P], F32, tag="bank")
+        for half in range(2):
+            nc.tensor.transpose(out=small_ps[:, half, :], in_=small_f[:, half, :], identity=ident[:])
+        small_t = consts.tile([P, 2, P], F32)
         nc.vector.tensor_copy(out=small_t[:], in_=small_ps[:])
-        b1_cols = small_t[:, 0, 0:PACK]
-        c_t = small_t[:, 1:3, 0:K]
-        b2_cols = small_t[:, 1:3, K]
+        c_t = small_t[:, :, 0:K]
+        b2_cols = small_t[:, :, K]
         c_minus2 = consts.tile([P, 2, K], F32)
         nc.vector.tensor_scalar_mul(out=c_minus2[:], in0=c_t, scalar1=-2.0)
         c_sq = consts.tile([P, 2, K], F32)
@@ -118,14 +120,10 @@ def tile_lintrans_pa_t_kernel(
 
         w1c = consts.tile([P, PACK, P], U32, align_bytes=64)
         nc.vector.tensor_copy(
-            out=w1c[:].bitcast(I32).rearrange("p s (a i) -> p s a i", i=PACK),
-            in_=w1_raw[:].bitcast(I32).rearrange("p (a s i) -> p s a i", s=PACK, i=PACK),
+            out=w1c[:].bitcast(I32), in_=w1_raw[:].bitcast(I32).rearrange("p (m t) -> p t m", t=PACK)
         )
         w1s = consts.tile([P, PACK, P], U8, align_bytes=64)
-        nc.vector.tensor_copy(
-            out=w1s[:].bitcast(I32),
-            in_=w1s_raw[:].bitcast(I32).rearrange("p (a s) -> p s a", s=PACK),
-        )
+        nc.vector.tensor_copy(out=w1s[:], in_=w1s_raw[:].rearrange("p (m t) -> p t m", t=PACK))
 
         z_norm = consts.tile([P, TILES], F32)
         q_sb = consts.tile([P, TILES, K], F32)
@@ -153,7 +151,6 @@ def tile_lintrans_pa_t_kernel(
         def first_matmul(g):
             codes, scales = x_quantised[g]
             h_t = work.tile([P, PACK, COLS], BF16)
-            rows = work.tile([P, PACK, COLS], BF16, name="h_rows")
             for s in range(PACK):
                 h_ps = banks.tile([P, COLS], F32, tag="bank")
                 nc.tensor.matmul_mx(
@@ -168,8 +165,7 @@ def tile_lintrans_pa_t_kernel(
                 nc.scalar.activation(
                     out=h_t[:, s, :], in_=h_ps[:], func=ACT.Silu, bias=b1_cols[:, s : s + 1], scale=1.0
                 )
-                nc.sync.dma_start(out=rows[s:P:PACK, :, :], in_=h_t[:, s, :])
-            h_rows[g] = rows
+            h_rows[g] = h_t
 
         def regroup_h(g):
             grouped = work.tile([P, COLS, PACK], BF16, align_bytes=64, name="h_grouped")
@@ -276,22 +272,22 @@ def tile_lintrans_pa_t_kernel(
         def is_group(g):
             return 0 <= g < GROUPS
 
-        for n in range(GROUPS + 6):
+        for n in range(GROUPS + 5):
             if is_group(n + AHEAD):
                 load_x(n + AHEAD)
             if is_group(n):
                 transpose_x(n)
-            if is_group(n - 3):
-                regroup_h(n - 3)
-            if is_group(n - 6) and (n - 6) % BATCH == BATCH - 1:
-                assign((n - 6) // BATCH)
+            if is_group(n - 2):
+                regroup_h(n - 2)
+            if is_group(n - 5) and (n - 5) % BATCH == BATCH - 1:
+                assign((n - 5) // BATCH)
             if is_group(n):
                 quantise_x(n)
             if is_group(n - 1):
                 first_matmul(n - 1)
+            if is_group(n - 2):
+                quantise_h(n - 2)
             if is_group(n - 3):
-                quantise_h(n - 3)
+                second_matmul(n - 3)
             if is_group(n - 4):
-                second_matmul(n - 4)
-            if is_group(n - 5):
-                distances(n - 5)
+                distances(n - 4)

@@ -17,11 +17,21 @@ P = 128
 PACK = 4
 ROWS, D_IN, H0, H1, K = 8192, 512, 512, 256, 20
 TILES = ROWS // P
-GROUP = 4
-GROUPS = TILES // GROUP
-COLS = GROUP * P
-AHEAD = 4
-BATCH = 2
+CFG = dict(
+    sizes=[1, 1, 2] + [4] * 14 + [2, 1, 1],
+    order="L-0 T0-0 X0-0 T1-0 X1-0 RG-2 a0-5 QX-0 a1-5 M0-1 S0-1 M1-1 S1-1 M2-1 S2-1 M3-1 S3-1 QH-2 a2-5 Z0-3 A0-3 a3-5 Z1-3 A1-3 a4-5 V0-3 W0-3 w0-3 a5-5 V1-3 W1-3 w1-3 SQ-4 d0-4 d1-4 d2-4 d3-4",
+    xc="AA",
+    zt="DA",
+    split=(1,),
+)
+
+SIZES = CFG['sizes']
+ORDER = [(w.split('-')[0], int(w.split('-')[1])) for w in CFG['order'].split()]
+O = CFG
+GROUPS = len(SIZES)
+FIRST = [sum(SIZES[:g]) for g in range(GROUPS)]
+AHEAD = CFG.get("ahead", 4)
+BATCH = CFG.get('batch', 8)
 
 FLOPS = 2 * ROWS * (D_IN * H0 + H0 * H1 + H1 * K)
 
@@ -38,18 +48,37 @@ def tile_lintrans_pa_t_kernel(
         consts = ctx.enter_context(tc.tile_pool(name="consts", bufs=1))
         x_pool = ctx.enter_context(tc.tile_pool(name="x_pool", bufs=AHEAD + 2))
         work = ctx.enter_context(tc.tile_pool(name="work", bufs=3))
-        banks = ctx.enter_context(tc.psum_pool(name="banks", bufs=7))
+        if O.get('pools'):
+            a, b, c = O['pools']
+            xbank = ctx.enter_context(tc.psum_pool(name="xbank", bufs=a))
+            hbank = ctx.enter_context(tc.psum_pool(name="hbank", bufs=b))
+            zbank = ctx.enter_context(tc.psum_pool(name="zbank", bufs=c))
+            XTAG, HTAG, ZTAG = "x", "h", "z"
+            banks = hbank
+            BT = "h"
+        else:
+            banks = ctx.enter_context(tc.psum_pool(name="banks", bufs=7))
+            xbank = hbank = zbank = banks
+            XTAG = HTAG = ZTAG = BT = "bank"
         dist_bank = ctx.enter_context(tc.psum_pool(name="dist_bank", bufs=1))
         ctx.enter_context(tc.manual_schedule())
 
         x_tiles, x_grouped, x_quantised = {}, {}, {}
         h_rows, h_grouped, h_quantised = {}, {}, {}
         z_tiles, z_transposed, dist_tiles = {}, {}, {}
+        x_trans, h_bank, z_bank, zt_bank = {}, {}, {}, {}
+
+        def tiles_of(g):
+            return slice(FIRST[g], FIRST[g] + SIZES[g])
 
         def load_x(g):
-            x_sb = x_pool.tile([P, GROUP, D_IN], BF16)
-            nc.sync.dma_start(out=x_sb[:], in_=x_rows[:, g * GROUP : (g + 1) * GROUP, :])
+            x_sb = x_pool.tile([P, SIZES[g], D_IN], BF16)
+            nc.sync.dma_start(out=x_sb[:], in_=x_rows[:, tiles_of(g), :])
             x_tiles[g] = x_sb
+
+        def load_more(g):
+            if AHEAD <= g + AHEAD < GROUPS:
+                load_x(g + AHEAD)
 
         w1s_raw = consts.tile([P, H0], U8, align_bytes=64)
         w2s = consts.tile([P, H1], U8, align_bytes=64)
@@ -97,7 +126,7 @@ def tile_lintrans_pa_t_kernel(
         nc.vector.tensor_copy(out=b1_cols[:], in_=b1_bf[:])
         small_f = consts.tile([P, 2, P], F32)
         nc.vector.tensor_copy(out=small_f[:], in_=small[:])
-        small_ps = banks.tile([P, 2, P], F32, tag="bank")
+        small_ps = banks.tile([P, 2, P], F32, tag=BT)
         for half in range(2):
             nc.tensor.transpose(out=small_ps[:, half, :], in_=small_f[:, half, :], identity=ident[:])
         small_t = consts.tile([P, 2, P], F32)
@@ -106,9 +135,12 @@ def tile_lintrans_pa_t_kernel(
         b2_cols = small_t[:, :, K]
         c_minus2 = consts.tile([P, 2, K], F32)
         nc.vector.tensor_scalar_mul(out=c_minus2[:], in0=c_t, scalar1=-2.0)
+        c_minus2_bf = consts.tile([P, 2, K], BF16)
+        if O['split']:
+            nc.vector.tensor_scalar_mul(out=c_minus2_bf[:], in0=c_t, scalar1=-2.0)
         c_sq = consts.tile([P, 2, K], F32)
         nc.vector.tensor_tensor(out=c_sq[:], in0=c_t, in1=c_t, op=ALU.mult)
-        c_norm_ps = banks.tile([P, K], F32, tag="bank")
+        c_norm_ps = banks.tile([P, K], F32, tag=BT)
         for half in range(2):
             nc.tensor.matmul(
                 out=c_norm_ps[:], lhsT=ones[:], rhs=c_sq[:, half, :], start=(half == 0), stop=(half == 1)
@@ -128,166 +160,242 @@ def tile_lintrans_pa_t_kernel(
         z_norm = consts.tile([P, TILES], F32)
         q_sb = consts.tile([P, TILES, K], F32)
 
-        def transpose_x(g):
-            grouped = work.tile([P, PACK * COLS], BF16, align_bytes=64, name="x_grouped")
-            grouped_words = grouped[:].bitcast(F32).rearrange("p (i r u) -> p i r u", i=GROUP, u=2)
-            for pair in range(2):
-                x_t = banks.tile([P, 2, 2, P], F32, tag="bank")
-                for i in range(2):
-                    words = x_tiles[g][:, 2 * pair + i, :].bitcast(F32)
-                    for u in range(2):
-                        nc.tensor.transpose(out=x_t[:, i, u, :], in_=words[:, u : D_IN // 2 : 2], identity=ident[:])
-                nc.scalar.copy(
-                    out=grouped_words[:, 2 * pair : 2 * pair + 2], in_=x_t[:].rearrange("p i u r -> p i r u")
-                )
-            x_grouped[g] = grouped
+        def transpose_x(g, f):
+            count = min(2, SIZES[g])
+            if 2 * f >= SIZES[g]:
+                return
+            x_t = xbank.tile([P, count, 2, P], F32, tag=XTAG)
+            for i in range(count):
+                words = x_tiles[g][:, 2 * f + i, :].bitcast(F32)
+                for u in range(2):
+                    nc.tensor.transpose(out=x_t[:, i, u, :], in_=words[:, u : D_IN // 2 : 2], identity=ident[:])
+            x_trans[g, f] = x_t
+
+        def copy_x(g, f):
+            if 2 * f >= SIZES[g]:
+                return
+            count = min(2, SIZES[g])
+            if f == 0:
+                grouped = work.tile([P, PACK * P * SIZES[g]], BF16, align_bytes=64, name="x_grouped")
+                x_grouped[g] = grouped
+            grouped_words = x_grouped[g][:].bitcast(F32).rearrange("p (i r u) -> p i r u", i=SIZES[g], u=2)
+            e = O['xc'][f]
+            src = x_trans[g, f][:].rearrange("p i u r -> p i r u")
+            if e == 'A':
+                nc.scalar.copy(out=grouped_words[:, 2 * f : 2 * f + count], in_=src)
+            else:
+                nc.vector.tensor_copy(out=grouped_words[:, 2 * f : 2 * f + count], in_=src)
 
         def quantise_x(g):
-            codes = work.tile([P, COLS], U32, align_bytes=64, name="x_codes")
-            scales = work.tile([P, COLS], U8, align_bytes=64, name="x_scales")
+            cols = SIZES[g] * P
+            codes = work.tile([P, cols], U32, align_bytes=64, name="x_codes")
+            scales = work.tile([P, cols], U8, align_bytes=64, name="x_scales")
             nc.vector.quantize_mx(out=codes[:].bitcast(FP8X4), scales=scales[:], in_=x_grouped[g][:])
             x_quantised[g] = (codes, scales)
 
-        def first_matmul(g):
+        def first_matmul(g, s):
             codes, scales = x_quantised[g]
-            h_t = work.tile([P, PACK, COLS], BF16)
-            for s in range(PACK):
-                h_ps = banks.tile([P, COLS], F32, tag="bank")
-                nc.tensor.matmul_mx(
-                    out=h_ps[:],
-                    lhsT=w1c[:, s, :].bitcast(FP8X4),
-                    lhsT_scale=w1s[:, s, :],
-                    rhs=codes[:].bitcast(FP8X4),
-                    rhs_scale=scales[:],
-                    start=True,
-                    stop=True,
-                )
-                nc.scalar.activation(
-                    out=h_t[:, s, :], in_=h_ps[:], func=ACT.Silu, bias=b1_cols[:, s : s + 1], scale=1.0
-                )
-            h_rows[g] = h_t
-
-        def regroup_h(g):
-            grouped = work.tile([P, COLS, PACK], BF16, align_bytes=64, name="h_grouped")
-            nc.vector.tensor_copy(
-                out=grouped[:].rearrange("p (c i) t -> p c t i", i=4),
-                in_=h_rows[g][:].rearrange("p t (c i) -> p c t i", i=4),
+            cols = SIZES[g] * P
+            h_ps = hbank.tile([P, cols], F32, tag=HTAG)
+            nc.tensor.matmul_mx(
+                out=h_ps[:],
+                lhsT=w1c[:, s, :].bitcast(FP8X4),
+                lhsT_scale=w1s[:, s, :],
+                rhs=codes[:].bitcast(FP8X4),
+                rhs_scale=scales[:],
+                start=True,
+                stop=True,
             )
-            h_grouped[g] = grouped
+            h_bank[g, s] = h_ps
+
+        def silu(g, s):
+            if s == 0:
+                h_t = work.tile([P, PACK, SIZES[g] * P], BF16)
+                h_rows[g] = h_t
+            nc.scalar.activation(
+                out=h_rows[g][:, s, :], in_=h_bank[g, s][:], func=ACT.Silu, bias=b1_cols[:, s : s + 1], scale=1.0
+            )
+
+        def regroup_h(g, part=0, parts=1):
+            if part == 0:
+                grouped = work.tile([P, SIZES[g] * P, PACK], BF16, align_bytes=64, name="h_grouped")
+                h_grouped[g] = grouped
+            n = SIZES[g] * P // parts
+            cols = slice(part * n, (part + 1) * n)
+            nc.vector.tensor_copy(
+                out=h_grouped[g][:, cols, :].rearrange("p (c i) t -> p c t i", i=4),
+                in_=h_rows[g][:, :, cols].rearrange("p t (c i) -> p c t i", i=4),
+            )
 
         def quantise_h(g):
-            codes = work.tile([P, COLS], U32, align_bytes=64, name="h_codes")
-            scales = work.tile([P, COLS], U8, align_bytes=64, name="h_scales")
+            cols = SIZES[g] * P
+            codes = work.tile([P, cols], U32, align_bytes=64, name="h_codes")
+            scales = work.tile([P, cols], U8, align_bytes=64, name="h_scales")
             nc.vector.quantize_mx(
                 out=codes[:].bitcast(FP8X4), scales=scales[:], in_=h_grouped[g][:].rearrange("p c t -> p (c t)")
             )
             h_quantised[g] = (codes, scales)
 
-        def second_matmul(g):
+        def second_matmul(g, f):
+            if 2 * f >= SIZES[g]:
+                return
             codes, scales = h_quantised[g]
-            z_sb = work.tile([P, GROUP, H1], F32)
-            for pair in range(2):
-                z_ps = banks.tile([P, 2, H1], F32, tag="bank")
-                for i in range(2):
-                    cols = slice((2 * pair + i) * P, (2 * pair + i + 1) * P)
-                    nc.tensor.matmul_mx(
-                        out=z_ps[:, i, :],
-                        lhsT=codes[:, cols].bitcast(FP8X4),
-                        lhsT_scale=scales[:, cols],
-                        rhs=w2c[:].bitcast(FP8X4),
-                        rhs_scale=w2s[:],
-                        start=True,
-                        stop=True,
-                    )
-                nc.vector.tensor_tensor(
-                    out=z_sb[:, 2 * pair : 2 * pair + 2, :],
-                    in0=z_ps[:],
-                    in1=b2_bc[:].unsqueeze(1).to_broadcast([P, 2, H1]),
-                    op=ALU.add,
-                )
-            nc.sync.dma_start(out=z_rows[:, g * GROUP : (g + 1) * GROUP, :], in_=z_sb[:])
-            z_tiles[g] = z_sb
-            z_t = work.tile([P, 2, COLS], F32)
-            for half in range(2):
-                z_t_ps = banks.tile([P, COLS], F32, tag="bank")
+            count = min(2, SIZES[g])
+            z_ps = zbank.tile([P, count, H1], F32, tag=ZTAG)
+            for i in range(count):
+                cols = slice((2 * f + i) * P, (2 * f + i + 1) * P)
                 nc.tensor.matmul_mx(
-                    out=z_t_ps[:],
-                    lhsT=w2c[:, half * P : (half + 1) * P].bitcast(FP8X4),
-                    lhsT_scale=w2s[:, half * P : (half + 1) * P],
-                    rhs=codes[:].bitcast(FP8X4),
-                    rhs_scale=scales[:],
+                    out=z_ps[:, i, :],
+                    lhsT=codes[:, cols].bitcast(FP8X4),
+                    lhsT_scale=scales[:, cols],
+                    rhs=w2c[:].bitcast(FP8X4),
+                    rhs_scale=w2s[:],
                     start=True,
                     stop=True,
                 )
-                if half == 0:
-                    nc.vector.tensor_scalar_add(out=z_t[:, half, :], in0=z_t_ps[:], scalar1=b2_cols[:, half : half + 1])
-                else:
-                    nc.scalar.activation(
-                        out=z_t[:, half, :], in_=z_t_ps[:], func=ACT.Identity, bias=b2_cols[:, half : half + 1], scale=1.0
-                    )
-            z_transposed[g] = z_t
+            z_bank[g, f] = z_ps
 
-        def distances(g):
-            for i in range(GROUP):
-                t = g * GROUP + i
-                squares = work.tile([P, H1], BF16)
-                nc.scalar.activation(
-                    out=squares[:], in_=z_tiles[g][:, i, :], func=ACT.Square, accum_out=z_norm[:, t : t + 1]
+        def add_b2(g, f):
+            if f == 0:
+                z_sb = work.tile([P, SIZES[g], H1], F32)
+                z_tiles[g] = z_sb
+            count = min(2, SIZES[g])
+            if 2 * f < SIZES[g]:
+                nc.vector.tensor_tensor(
+                    out=z_tiles[g][:, 2 * f : 2 * f + count, :],
+                    in0=z_bank[g, f][:],
+                    in1=b2_bc[:].unsqueeze(1).to_broadcast([P, count, H1]),
+                    op=ALU.add,
                 )
-            if g % BATCH == 0:
-                dist_ps = dist_bank.tile([P, BATCH * GROUP, K], F32)
-                dist_tiles[g // BATCH] = dist_ps
-            for i in range(GROUP):
-                for half in range(2):
-                    nc.tensor.matmul(
-                        out=dist_tiles[g // BATCH][:, (g % BATCH) * GROUP + i, :],
-                        lhsT=z_transposed[g][:, half, i * P : (i + 1) * P],
-                        rhs=c_minus2[:, half, :],
-                        start=(half == 0),
-                        stop=(half == 1),
+            if f == 1:
+                nc.sync.dma_start(out=z_rows[:, tiles_of(g), :], in_=z_tiles[g][:])
+
+        def second_transposed(g, half):
+            codes, scales = h_quantised[g]
+            z_t_ps = zbank.tile([P, SIZES[g] * P], F32, tag=ZTAG)
+            nc.tensor.matmul_mx(
+                out=z_t_ps[:],
+                lhsT=w2c[:, half * P : (half + 1) * P].bitcast(FP8X4),
+                lhsT_scale=w2s[:, half * P : (half + 1) * P],
+                rhs=codes[:].bitcast(FP8X4),
+                rhs_scale=scales[:],
+                start=True,
+                stop=True,
+            )
+            zt_bank[g, half] = z_t_ps
+
+        def copy_zt(g, half, part=0):
+            z_t_ps = zt_bank[g, half]
+            bias = b2_cols[:, half : half + 1]
+            if half not in O['split']:
+                if part == 1:
+                    return
+                z_t = work.tile([P, SIZES[g] * P], F32, name="z_t%d" % half)
+                z_transposed[g, half] = (z_t,)
+                if O['zt'][half] == 'D':
+                    nc.vector.tensor_scalar_add(out=z_t[:], in0=z_t_ps[:], scalar1=bias)
+                else:
+                    nc.scalar.activation(out=z_t[:], in_=z_t_ps[:], func=ACT.Identity, bias=bias, scale=1.0)
+            elif part == 0:
+                hi = work.tile([P, SIZES[g] * P], BF16, name="z_hi%d" % half)
+                nc.scalar.activation(out=hi[:], in_=z_t_ps[:], func=ACT.Identity, bias=bias, scale=1.0)
+                z_transposed[g, half] = (hi,)
+            else:
+                lo = work.tile([P, SIZES[g] * P], BF16, name="z_lo%d" % half)
+                hi = z_transposed[g, half][0]
+                nc.vector.scalar_tensor_tensor(
+                    out=lo[:], in0=z_t_ps[:], scalar=bias, in1=hi[:], op0=ALU.add, op1=ALU.subtract
+                )
+                z_transposed[g, half] = (hi, lo)
+
+        def norms(g, lo=0, hi=4):
+            for i in range(lo, min(hi, SIZES[g])):
+                t = FIRST[g] + i
+                squares = work.tile([P, H1], BF16)
+                if O.get('sq', 'A') == 'A':
+                    nc.scalar.activation(
+                        out=squares[:], in_=z_tiles[g][:, i, :], func=ACT.Square, accum_out=z_norm[:, t : t + 1]
+                    )
+                else:
+                    nc.vector.scalar_tensor_tensor(
+                        out=squares[:], in0=z_tiles[g][:, i, :], scalar=1.0, in1=z_tiles[g][:, i, :], op0=ALU.mult, op1=ALU.mult,
+                        accum_out=z_norm[:, t : t + 1]
                     )
 
-        def assign(batch):
-            n = BATCH * GROUP
-            tiles = slice(batch * n, (batch + 1) * n)
-            shape = [P, n, K]
-            denom = work.tile(shape, F32)
-            nc.vector.tensor_tensor(
-                out=denom[:], in0=dist_tiles[batch][:], in1=c_norm1[:].unsqueeze(1).to_broadcast(shape), op=ALU.add
-            )
-            nc.vector.tensor_tensor(
-                out=denom[:], in0=denom[:], in1=z_norm[:, tiles].unsqueeze(2).to_broadcast(shape), op=ALU.add
-            )
-            kernel = work.tile(shape, F32)
-            nc.vector.reciprocal(out=kernel[:], in_=denom[:])
-            total = work.tile([P, n], F32)
-            nc.vector.tensor_reduce(out=total[:], in_=kernel[:], axis=AXIS.X, op=ALU.add)
-            inverse = work.tile([P, n], F32)
-            nc.vector.reciprocal(out=inverse[:], in_=total[:])
-            nc.vector.tensor_tensor(
-                out=q_sb[:, tiles, :], in0=kernel[:], in1=inverse[:].unsqueeze(2).to_broadcast(shape), op=ALU.mult
-            )
-            nc.sync.dma_start(out=q_rows[:, tiles, :], in_=q_sb[:, tiles, :])
+        kernels = {}
+
+        def assign(batch, k):
+            tiles = slice(batch * BATCH, (batch + 1) * BATCH)
+            shape = [P, BATCH, K]
+            if k == 0:
+                denom = work.tile(shape, F32)
+                nc.vector.tensor_tensor(
+                    out=denom[:], in0=dist_tiles[batch][:], in1=c_norm1[:].unsqueeze(1).to_broadcast(shape), op=ALU.add
+                )
+                kernels[batch, k] = denom
+            if k == 1:
+                denom2 = work.tile(shape, F32)
+                nc.vector.tensor_tensor(
+                    out=denom2[:], in0=kernels[batch, 0][:], in1=z_norm[:, tiles].unsqueeze(2).to_broadcast(shape), op=ALU.add
+                )
+                kernels[batch, k] = denom2
+            if k == 2:
+                kernel = work.tile(shape, F32)
+                nc.vector.reciprocal(out=kernel[:], in_=kernels[batch, 1][:])
+                kernels[batch, k] = kernel
+            if k == 3:
+                total = work.tile([P, BATCH], F32)
+                nc.vector.tensor_reduce(out=total[:], in_=kernels[batch, 2][:], axis=AXIS.X, op=ALU.add)
+                kernels[batch, k] = total
+            if k == 4:
+                inverse = work.tile([P, BATCH], F32)
+                nc.vector.reciprocal(out=inverse[:], in_=kernels[batch, 3][:])
+                kernels[batch, k] = inverse
+            if k == 5:
+                nc.vector.tensor_tensor(
+                    out=q_sb[:, tiles, :], in0=kernels[batch, 2][:], in1=kernels[batch, 4][:].unsqueeze(2).to_broadcast(shape), op=ALU.mult
+                )
+                nc.sync.dma_start(out=q_rows[:, tiles, :], in_=q_sb[:, tiles, :])
 
         def is_group(g):
             return 0 <= g < GROUPS
 
-        for n in range(GROUPS + 5):
-            if is_group(n + AHEAD):
-                load_x(n + AHEAD)
-            if is_group(n):
-                transpose_x(n)
-            if is_group(n - 2):
-                regroup_h(n - 2)
-            if is_group(n - 5) and (n - 5) % BATCH == BATCH - 1:
-                assign((n - 5) // BATCH)
-            if is_group(n):
-                quantise_x(n)
-            if is_group(n - 1):
-                first_matmul(n - 1)
-            if is_group(n - 2):
-                quantise_h(n - 2)
-            if is_group(n - 3):
-                second_matmul(n - 3)
-            if is_group(n - 4):
-                distances(n - 4)
+        def step(k):
+            return lambda g: assign(FIRST[g] // BATCH, k) if (FIRST[g] + SIZES[g]) % BATCH == 0 else None
+
+        def products(g, i):
+            batch = FIRST[g] // BATCH
+            if FIRST[g] % BATCH == 0 and i == 0:
+                dist_ps = dist_bank.tile([P, BATCH, K], F32)
+                dist_tiles[batch] = dist_ps
+            if i < SIZES[g]:
+                ops = [(t, half) for half in range(2) for t in z_transposed[g, half]]
+                for m, (t, half) in enumerate(ops):
+                    nc.tensor.matmul(
+                        out=dist_tiles[batch][:, FIRST[g] % BATCH + i, :],
+                        lhsT=t[:, i * P : (i + 1) * P],
+                        rhs=(c_minus2_bf if half in O["split"] else c_minus2)[:, half, :],
+                        start=(m == 0),
+                        stop=(m == len(ops) - 1),
+                    )
+
+        fns = dict(
+            L=load_more, T0=lambda g: transpose_x(g, 0), T1=lambda g: transpose_x(g, 1), X0=lambda g: copy_x(g, 0), X1=lambda g: copy_x(g, 1),
+            QX=quantise_x, RG=regroup_h, RA=lambda g: regroup_h(g, 0, 2), RB=lambda g: regroup_h(g, 1, 2), QH=quantise_h,
+            Z0=lambda g: second_matmul(g, 0), Z1=lambda g: second_matmul(g, 1), A0=lambda g: add_b2(g, 0), A1=lambda g: add_b2(g, 1),
+            V0=lambda g: second_transposed(g, 0), V1=lambda g: second_transposed(g, 1),
+            W0=lambda g: copy_zt(g, 0), W1=lambda g: copy_zt(g, 1), w0=lambda g: copy_zt(g, 0, 1), w1=lambda g: copy_zt(g, 1, 1),
+            SQ=norms, SA=lambda g: norms(g, 0, 2), SB=lambda g: norms(g, 2, 4), SQ0=lambda g: norms(g, 0, 1),
+        )
+        for s in range(4):
+            fns["M%d" % s] = lambda g, s=s: first_matmul(g, s)
+            fns["d%d" % s] = lambda g, s=s: products(g, s)
+            fns["q%d" % s] = lambda g, s=s: norms(g, s, s + 1)
+            fns["S%d" % s] = lambda g, s=s: silu(g, s)
+        for s in range(6):
+            fns["a%d" % s] = step(s)
+        depth = max(lag for name, lag in ORDER)
+        for n in range(GROUPS + depth):
+            for name, lag in ORDER:
+                if is_group(n - lag):
+                    fns[name](n - lag)

@@ -18,11 +18,12 @@ PACK = 4
 ROWS, D_IN, H0, H1, K = 8192, 512, 512, 256, 20
 TILES = ROWS // P
 CFG = dict(
-    sizes=[1, 1, 2] + [4] * 14 + [2, 1, 1],
-    order="L-0 T0-0 X0-0 T1-0 X1-0 RG-2 a0-5 QX-0 a1-5 M0-1 S0-1 M1-1 S1-1 M2-1 S2-1 M3-1 S3-1 QH-2 a2-5 Z0-3 A0-3 a3-5 Z1-3 A1-3 a4-5 V0-3 W0-3 w0-3 a5-5 V1-3 W1-3 w1-3 SQ-4 d0-4 d1-4 d2-4 d3-4",
+    sizes=[4] * 15 + [2, 2],
+    order="L-0 T0-0 X0-0 T1-0 X1-0 RG-2 a0-5 QX-0 k1-0 k4-2 a1-5 M0-1 S0-1 M1-1 S1-1 M2-1 S2-1 M3-1 S3-1 k3-1 QH-2 k2-0 a2-5 Z0-3 A0-3 a3-5 Z1-3 A1-3 a4-5 V0-3 W0-3 w0-3 a5-5 V1-3 W1-3 w1-3 SQ-4 d0-4 d1-4 d2-4 d3-4",
     xc="AA",
     zt="DA",
     split=(1,),
+    za=3,
 )
 
 SIZES = CFG['sizes']
@@ -81,18 +82,14 @@ def tile_lintrans_pa_t_kernel(
                 load_x(g + AHEAD)
 
         w1s_raw = consts.tile([P, H0], U8, align_bytes=64)
-        w2s = consts.tile([P, H1], U8, align_bytes=64)
+        nc.vector.memset(w1s_raw[:].bitcast(I32), 0)
         small = consts.tile([P, 2, P], BF16)
         nc.vector.memset(small[:], 0.0)
-        nc.vector.memset(w1s_raw[:].bitcast(I32), 0)
+        w2s = consts.tile([P, H1], U8, align_bytes=64)
         nc.vector.memset(w2s[:].bitcast(I32), 0)
+        ident = consts.tile([P, P], F32)
+        make_identity(nc, ident[:])
 
-        b1_bf = consts.tile([P, PACK], BF16)
-        nc.sync.dma_start(out=b1_bf[:], in_=b1.rearrange("(m t) -> m t", t=PACK))
-        nc.sync.dma_start(out=small[0:K, :, :], in_=clusters.rearrange("k (h j) -> k h j", h=2))
-        nc.sync.dma_start(out=small[K : K + 1, :, :], in_=b2.rearrange("(o h j) -> o h j", o=1, h=2))
-        b2_bf = consts.tile([P, H1], BF16)
-        nc.sync.dma_start(out=b2_bf[:], in_=b2.partition_broadcast(P))
         load_x(0)
         w1_raw = consts.tile([P, H0], U32, align_bytes=64)
         nc.sync.dma_start(
@@ -104,7 +101,11 @@ def tile_lintrans_pa_t_kernel(
                 out=w1s_raw[32 * quad : 32 * quad + 4, :].bitcast(I32),
                 in_=W1_scales[0, 4 * quad : 4 * quad + 4, :].bitcast(I32),
             )
+        b1_bf = consts.tile([P, PACK], BF16)
+        nc.gpsimd.dma_start(out=b1_bf[:], in_=b1.rearrange("(m t) -> m t", t=PACK))
         load_x(1)
+        nc.sync.dma_start(out=small[0:K, :, :], in_=clusters.rearrange("k (h j) -> k h j", h=2))
+        nc.sync.dma_start(out=small[K : K + 1, :, :], in_=b2.rearrange("(o h j) -> o h j", o=1, h=2))
         w2c = consts.tile([P, H1], U32, align_bytes=64)
         nc.sync.dma_start(
             out=w2c[:].bitcast(I32),
@@ -118,44 +119,58 @@ def tile_lintrans_pa_t_kernel(
         for g in range(2, AHEAD):
             load_x(g)
 
-        ident = consts.tile([P, P], F32)
-        make_identity(nc, ident[:])
-        ones = consts.tile([P, P], F32)
-        nc.vector.memset(ones[:], 1.0)
-        b1_cols = consts.tile([P, PACK], F32)
-        nc.vector.tensor_copy(out=b1_cols[:], in_=b1_bf[:])
-        small_f = consts.tile([P, 2, P], F32)
-        nc.vector.tensor_copy(out=small_f[:], in_=small[:])
-        small_ps = banks.tile([P, 2, P], F32, tag=BT)
-        for half in range(2):
-            nc.tensor.transpose(out=small_ps[:, half, :], in_=small_f[:, half, :], identity=ident[:])
-        small_t = consts.tile([P, 2, P], F32)
-        nc.vector.tensor_copy(out=small_t[:], in_=small_ps[:])
-        c_t = small_t[:, :, 0:K]
-        b2_cols = small_t[:, :, K]
-        c_minus2 = consts.tile([P, 2, K], F32)
-        nc.vector.tensor_scalar_mul(out=c_minus2[:], in0=c_t, scalar1=-2.0)
-        c_minus2_bf = consts.tile([P, 2, K], BF16)
-        if O['split']:
-            nc.vector.tensor_scalar_mul(out=c_minus2_bf[:], in0=c_t, scalar1=-2.0)
-        c_sq = consts.tile([P, 2, K], F32)
-        nc.vector.tensor_tensor(out=c_sq[:], in0=c_t, in1=c_t, op=ALU.mult)
-        c_norm_ps = banks.tile([P, K], F32, tag=BT)
-        for half in range(2):
-            nc.tensor.matmul(
-                out=c_norm_ps[:], lhsT=ones[:], rhs=c_sq[:, half, :], start=(half == 0), stop=(half == 1)
-            )
-        c_norm1 = consts.tile([P, K], F32)
-        nc.vector.tensor_scalar_add(out=c_norm1[:], in0=c_norm_ps[:], scalar1=1.0)
-        b2_bc = consts.tile([P, H1], F32)
-        nc.vector.tensor_copy(out=b2_bc[:], in_=b2_bf[:])
-
         w1c = consts.tile([P, PACK, P], U32, align_bytes=64)
         nc.vector.tensor_copy(
             out=w1c[:].bitcast(I32), in_=w1_raw[:].bitcast(I32).rearrange("p (m t) -> p t m", t=PACK)
         )
         w1s = consts.tile([P, PACK, P], U8, align_bytes=64)
         nc.vector.tensor_copy(out=w1s[:], in_=w1s_raw[:].rearrange("p (m t) -> p t m", t=PACK))
+        b1_cols = consts.tile([P, PACK], F32)
+        nc.vector.tensor_copy(out=b1_cols[:], in_=b1_bf[:])
+
+        small_f = consts.tile([P, 2, P], F32)
+        small_t = consts.tile([P, 2, P], F32)
+        c_t = small_t[:, :, 0:K]
+        b2_cols = small_t[:, :, K]
+        b2_bc = consts.tile([P, H1], F32)
+        c_minus2 = consts.tile([P, 2, K], F32)
+        c_minus2_bf = consts.tile([P, 2, K], BF16)
+        c_sq = consts.tile([P, H1], F32)
+        c_len = consts.tile([P, 1], F32)
+        c_diag = consts.tile([P, K], F32)
+        c_norm1 = consts.tile([P, K], F32)
+        ones = consts.tile([P, P], F32)
+        row = consts.tile([P, P], F32)
+
+        const_ps = {}
+
+        def constants(k):
+            if k == 1:
+                nc.gpsimd.memset(ones[:], 1.0)
+                nc.vector.tensor_copy(out=small_f[:], in_=small[:])
+                nc.vector.tensor_scalar_mul(out=row[:], in0=ones[:], scalar1=ident[:, K : K + 1])
+                flat = small_f[:].rearrange("p h j -> p (h j)")
+                nc.vector.scalar_tensor_tensor(
+                    out=c_sq[:], in0=flat, scalar=1.0, in1=flat, op0=ALU.mult, op1=ALU.mult, accum_out=c_len[:]
+                )
+            if k == 2:
+                nc.vector.tensor_scalar_mul(out=c_diag[:], in0=ident[:, 0:K], scalar1=c_len[:])
+            if k == 3:
+                small_ps = banks.tile([P, 2, P], F32, tag=BT)
+                for half in range(2):
+                    nc.tensor.transpose(out=small_ps[:, half, :], in_=small_f[:, half, :], identity=ident[:])
+                b2_ps = banks.tile([P, H1 + K], F32, tag=BT)
+                nc.tensor.matmul(out=b2_ps[:, 0:H1], lhsT=row[:], rhs=small_f[:].rearrange("p h j -> p (h j)"), start=True, stop=True)
+                nc.tensor.matmul(out=b2_ps[:, H1:], lhsT=ones[:], rhs=c_diag[:], start=True, stop=True)
+                const_ps[0] = small_ps
+                const_ps[1] = b2_ps
+            if k == 4:
+                nc.vector.tensor_copy(out=small_t[:], in_=const_ps[0][:])
+                nc.vector.tensor_copy(out=b2_bc[:], in_=const_ps[1][:, 0:H1])
+                nc.vector.tensor_scalar_add(out=c_norm1[:], in0=const_ps[1][:, H1:], scalar1=1.0)
+                nc.vector.tensor_scalar_mul(out=c_minus2[:], in0=c_t, scalar1=-2.0)
+                if O["split"]:
+                    nc.vector.tensor_scalar_mul(out=c_minus2_bf[:], in0=c_t, scalar1=-2.0)
 
         z_norm = consts.tile([P, TILES], F32)
         q_sb = consts.tile([P, TILES, K], F32)
@@ -179,7 +194,7 @@ def tile_lintrans_pa_t_kernel(
                 grouped = work.tile([P, PACK * P * SIZES[g]], BF16, align_bytes=64, name="x_grouped")
                 x_grouped[g] = grouped
             grouped_words = x_grouped[g][:].bitcast(F32).rearrange("p (i r u) -> p i r u", i=SIZES[g], u=2)
-            e = O['xc'][f]
+            e = 'D' if g < O.get('xd', 0) else O['xc'][f]
             src = x_trans[g, f][:].rearrange("p i u r -> p i r u")
             if e == 'A':
                 nc.scalar.copy(out=grouped_words[:, 2 * f : 2 * f + count], in_=src)
@@ -284,15 +299,18 @@ def tile_lintrans_pa_t_kernel(
             )
             zt_bank[g, half] = z_t_ps
 
+        def splits(g):
+            return O['split'] if g < GROUPS - O.get('sa', 0) else ()
+
         def copy_zt(g, half, part=0):
             z_t_ps = zt_bank[g, half]
             bias = b2_cols[:, half : half + 1]
-            if half not in O['split']:
+            if half not in splits(g):
                 if part == 1:
                     return
                 z_t = work.tile([P, SIZES[g] * P], F32, name="z_t%d" % half)
                 z_transposed[g, half] = (z_t,)
-                if O['zt'][half] == 'D':
+                if O['zt'][half] == 'D' and g < GROUPS - O.get('za', 0):
                     nc.vector.tensor_scalar_add(out=z_t[:], in0=z_t_ps[:], scalar1=bias)
                 else:
                     nc.scalar.activation(out=z_t[:], in_=z_t_ps[:], func=ACT.Identity, bias=bias, scale=1.0)
@@ -330,13 +348,16 @@ def tile_lintrans_pa_t_kernel(
             if k == 0:
                 denom = work.tile(shape, F32)
                 nc.vector.tensor_tensor(
-                    out=denom[:], in0=dist_tiles[batch][:], in1=c_norm1[:].unsqueeze(1).to_broadcast(shape), op=ALU.add
+                    out=denom[:],
+                    in0=z_norm[:, tiles].unsqueeze(2).to_broadcast(shape),
+                    in1=c_norm1[:].unsqueeze(1).to_broadcast(shape),
+                    op=ALU.add,
                 )
                 kernels[batch, k] = denom
             if k == 1:
                 denom2 = work.tile(shape, F32)
                 nc.vector.tensor_tensor(
-                    out=denom2[:], in0=kernels[batch, 0][:], in1=z_norm[:, tiles].unsqueeze(2).to_broadcast(shape), op=ALU.add
+                    out=denom2[:], in0=dist_tiles[batch][:], in1=kernels[batch, 0][:], op=ALU.add
                 )
                 kernels[batch, k] = denom2
             if k == 2:
@@ -374,13 +395,13 @@ def tile_lintrans_pa_t_kernel(
                     nc.tensor.matmul(
                         out=dist_tiles[batch][:, FIRST[g] % BATCH + i, :],
                         lhsT=t[:, i * P : (i + 1) * P],
-                        rhs=(c_minus2_bf if half in O["split"] else c_minus2)[:, half, :],
+                        rhs=(c_minus2_bf if half in splits(g) else c_minus2)[:, half, :],
                         start=(m == 0),
                         stop=(m == len(ops) - 1),
                     )
 
         fns = dict(
-            L=load_more, T0=lambda g: transpose_x(g, 0), T1=lambda g: transpose_x(g, 1), X0=lambda g: copy_x(g, 0), X1=lambda g: copy_x(g, 1),
+            L=load_more,  T0=lambda g: transpose_x(g, 0), T1=lambda g: transpose_x(g, 1), X0=lambda g: copy_x(g, 0), X1=lambda g: copy_x(g, 1),
             QX=quantise_x, RG=regroup_h, RA=lambda g: regroup_h(g, 0, 2), RB=lambda g: regroup_h(g, 1, 2), QH=quantise_h,
             Z0=lambda g: second_matmul(g, 0), Z1=lambda g: second_matmul(g, 1), A0=lambda g: add_b2(g, 0), A1=lambda g: add_b2(g, 1),
             V0=lambda g: second_transposed(g, 0), V1=lambda g: second_transposed(g, 1),
@@ -392,6 +413,8 @@ def tile_lintrans_pa_t_kernel(
             fns["d%d" % s] = lambda g, s=s: products(g, s)
             fns["q%d" % s] = lambda g, s=s: norms(g, s, s + 1)
             fns["S%d" % s] = lambda g, s=s: silu(g, s)
+        for s in range(1, 5):
+            fns["k%d" % s] = lambda g, s=s: constants(s) if g == 0 else None
         for s in range(6):
             fns["a%d" % s] = step(s)
         depth = max(lag for name, lag in ORDER)

@@ -18,12 +18,16 @@ PACK = 4
 ROWS, D_IN, H0, H1, K = 8192, 512, 512, 256, 20
 TILES = ROWS // P
 CFG = dict(
-    sizes=[4] * 15 + [2, 2],
-    order="L-0 T0-0 X0-0 T1-0 X1-0 RG-2 a0-5 QX-0 k1-0 k4-2 a1-5 M0-1 S0-1 M1-1 S1-1 M2-1 S2-1 M3-1 S3-1 k3-1 QH-2 k2-0 a2-5 Z0-3 A0-3 a3-5 Z1-3 A1-3 a4-5 V0-3 W0-3 w0-3 a5-5 V1-3 W1-3 w1-3 SQ-4 d0-4 d1-4 d2-4 d3-4",
+    sizes=[4] * 16,
+    order="L-0 T0-0 X0-0 T1-0 X1-0 RG-2 a0-5 QX-0 k1-0 a1-5 M0-1 S0-1 M1-1 S1-1 M2-1 S2-1 M3-1 S3-1 k3-1 k4-1 QH-2 k2-0 a2-5 Z0-3 A0-3 a3-5 Z1-3 A1-3 a4-5 V0-3 W0-3 w0-3 a5-5 V1-3 W1-3 w1-3 SQ-4 d0-4 d1-4 d2-4 d3-4",
     xc="AA",
     zt="DA",
     split=(1,),
     za=3,
+    gq=1,
+    xfirst=1,
+    xsplit=1,
+    ag=(0, 5),
 )
 
 SIZES = CFG['sizes']
@@ -32,7 +36,8 @@ O = CFG
 GROUPS = len(SIZES)
 FIRST = [sum(SIZES[:g]) for g in range(GROUPS)]
 AHEAD = CFG.get("ahead", 4)
-BATCH = CFG.get('batch', 8)
+BATCHES = CFG.get('batches', [8] * 8)
+BFIRST = [sum(BATCHES[:b]) for b in range(len(BATCHES))]
 
 FLOPS = 2 * ROWS * (D_IN * H0 + H0 * H1 + H1 * K)
 
@@ -74,7 +79,11 @@ def tile_lintrans_pa_t_kernel(
 
         def load_x(g):
             x_sb = x_pool.tile([P, SIZES[g], D_IN], BF16)
-            nc.sync.dma_start(out=x_sb[:], in_=x_rows[:, tiles_of(g), :])
+            step = 2 if g < O.get('xsplit', 0) else SIZES[g]
+            for i in range(0, SIZES[g], step):
+                nc.sync.dma_start(
+                    out=x_sb[:, i : i + step, :], in_=x_rows[:, FIRST[g] + i : FIRST[g] + i + step, :]
+                )
             x_tiles[g] = x_sb
 
         def load_more(g):
@@ -91,6 +100,8 @@ def tile_lintrans_pa_t_kernel(
         make_identity(nc, ident[:])
 
         load_x(0)
+        if O.get('xfirst'):
+            load_x(1)
         w1_raw = consts.tile([P, H0], U32, align_bytes=64)
         nc.sync.dma_start(
             out=w1_raw[:].bitcast(I32),
@@ -103,9 +114,10 @@ def tile_lintrans_pa_t_kernel(
             )
         b1_bf = consts.tile([P, PACK], BF16)
         nc.gpsimd.dma_start(out=b1_bf[:], in_=b1.rearrange("(m t) -> m t", t=PACK))
-        load_x(1)
-        nc.sync.dma_start(out=small[0:K, :, :], in_=clusters.rearrange("k (h j) -> k h j", h=2))
-        nc.sync.dma_start(out=small[K : K + 1, :, :], in_=b2.rearrange("(o h j) -> o h j", o=1, h=2))
+        if not O.get('xfirst'):
+            load_x(1)
+        (nc.gpsimd if O.get('gq') else nc.sync).dma_start(out=small[0:K, :, :], in_=clusters.rearrange("k (h j) -> k h j", h=2))
+        (nc.gpsimd if O.get('gq') else nc.sync).dma_start(out=small[K : K + 1, :, :], in_=b2.rearrange("(o h j) -> o h j", o=1, h=2))
         w2c = consts.tile([P, H1], U32, align_bytes=64)
         nc.sync.dma_start(
             out=w2c[:].bitcast(I32),
@@ -314,6 +326,22 @@ def tile_lintrans_pa_t_kernel(
                     nc.vector.tensor_scalar_add(out=z_t[:], in0=z_t_ps[:], scalar1=bias)
                 else:
                     nc.scalar.activation(out=z_t[:], in_=z_t_ps[:], func=ACT.Identity, bias=bias, scale=1.0)
+            elif half in O.get('gp', ()):
+                if part == 1:
+                    return
+                z_t = work.tile([P, SIZES[g] * P], F32, name="z_t%d" % half)
+                if O['zt'][half] == 'D':
+                    nc.vector.tensor_scalar_add(out=z_t[:], in0=z_t_ps[:], scalar1=bias)
+                else:
+                    nc.scalar.activation(out=z_t[:], in_=z_t_ps[:], func=ACT.Identity, bias=bias, scale=1.0)
+                hi = work.tile([P, SIZES[g] * P], BF16, name="z_hi%d" % half)
+                lo = work.tile([P, SIZES[g] * P], BF16, name="z_lo%d" % half)
+                n = min(O.get('gcols', 512), SIZES[g] * P)
+                for c0 in range(0, SIZES[g] * P, n):
+                    cs = slice(c0, c0 + n)
+                    nc.gpsimd.tensor_scalar(out=hi[:, cs], in0=z_t[:, cs], scalar1=1.0, scalar2=0.0, op0=ALU.mult, op1=ALU.add)
+                    nc.gpsimd.tensor_tensor(out=lo[:, cs], in0=z_t[:, cs], in1=hi[:, cs], op=ALU.subtract)
+                z_transposed[g, half] = (hi, lo)
             elif part == 0:
                 hi = work.tile([P, SIZES[g] * P], BF16, name="z_hi%d" % half)
                 nc.scalar.activation(out=hi[:], in_=z_t_ps[:], func=ACT.Identity, bias=bias, scale=1.0)
@@ -330,7 +358,7 @@ def tile_lintrans_pa_t_kernel(
             for i in range(lo, min(hi, SIZES[g])):
                 t = FIRST[g] + i
                 squares = work.tile([P, H1], BF16)
-                if O.get('sq', 'A') == 'A':
+                if not (O.get('sqd') and g % O['sqd'] == 1 and i == SIZES[g] - 1 and 0 < g < GROUPS - 2):
                     nc.scalar.activation(
                         out=squares[:], in_=z_tiles[g][:, i, :], func=ACT.Square, accum_out=z_norm[:, t : t + 1]
                     )
@@ -342,12 +370,15 @@ def tile_lintrans_pa_t_kernel(
 
         kernels = {}
 
+        def batch_of(g):
+            return max(b for b in range(len(BATCHES)) if BFIRST[b] <= FIRST[g])
+
         def assign(batch, k):
-            tiles = slice(batch * BATCH, (batch + 1) * BATCH)
-            shape = [P, BATCH, K]
+            tiles = slice(BFIRST[batch], BFIRST[batch] + BATCHES[batch])
+            shape = [P, BATCHES[batch], K]
             if k == 0:
                 denom = work.tile(shape, F32)
-                nc.vector.tensor_tensor(
+                (nc.gpsimd if 0 in O.get('ag', ()) else nc.vector).tensor_tensor(
                     out=denom[:],
                     in0=z_norm[:, tiles].unsqueeze(2).to_broadcast(shape),
                     in1=c_norm1[:].unsqueeze(1).to_broadcast(shape),
@@ -365,15 +396,15 @@ def tile_lintrans_pa_t_kernel(
                 nc.vector.reciprocal(out=kernel[:], in_=kernels[batch, 1][:])
                 kernels[batch, k] = kernel
             if k == 3:
-                total = work.tile([P, BATCH], F32)
+                total = work.tile([P, BATCHES[batch]], F32)
                 nc.vector.tensor_reduce(out=total[:], in_=kernels[batch, 2][:], axis=AXIS.X, op=ALU.add)
                 kernels[batch, k] = total
             if k == 4:
-                inverse = work.tile([P, BATCH], F32)
+                inverse = work.tile([P, BATCHES[batch]], F32)
                 nc.vector.reciprocal(out=inverse[:], in_=kernels[batch, 3][:])
                 kernels[batch, k] = inverse
             if k == 5:
-                nc.vector.tensor_tensor(
+                (nc.gpsimd if 5 in O.get('ag', ()) and batch < len(BATCHES) - 1 else nc.vector).tensor_tensor(
                     out=q_sb[:, tiles, :], in0=kernels[batch, 2][:], in1=kernels[batch, 4][:].unsqueeze(2).to_broadcast(shape), op=ALU.mult
                 )
                 nc.sync.dma_start(out=q_rows[:, tiles, :], in_=q_sb[:, tiles, :])
@@ -382,18 +413,18 @@ def tile_lintrans_pa_t_kernel(
             return 0 <= g < GROUPS
 
         def step(k):
-            return lambda g: assign(FIRST[g] // BATCH, k) if (FIRST[g] + SIZES[g]) % BATCH == 0 else None
+            return lambda g: assign(batch_of(g), k) if FIRST[g] + SIZES[g] == BFIRST[batch_of(g)] + BATCHES[batch_of(g)] else None
 
         def products(g, i):
-            batch = FIRST[g] // BATCH
-            if FIRST[g] % BATCH == 0 and i == 0:
-                dist_ps = dist_bank.tile([P, BATCH, K], F32)
+            batch = batch_of(g)
+            if FIRST[g] == BFIRST[batch] and i == 0:
+                dist_ps = dist_bank.tile([P, BATCHES[batch], K], F32)
                 dist_tiles[batch] = dist_ps
             if i < SIZES[g]:
                 ops = [(t, half) for half in range(2) for t in z_transposed[g, half]]
                 for m, (t, half) in enumerate(ops):
                     nc.tensor.matmul(
-                        out=dist_tiles[batch][:, FIRST[g] % BATCH + i, :],
+                        out=dist_tiles[batch][:, FIRST[g] - BFIRST[batch] + i, :],
                         lhsT=t[:, i * P : (i + 1) * P],
                         rhs=(c_minus2_bf if half in splits(g) else c_minus2)[:, half, :],
                         start=(m == 0),
@@ -418,7 +449,15 @@ def tile_lintrans_pa_t_kernel(
         for s in range(6):
             fns["a%d" % s] = step(s)
         depth = max(lag for name, lag in ORDER)
+        def late(name):
+            return name[0] in "ZAVWwSdqa" and name not in ("S0", "S1", "S2", "S3")
+
         for n in range(GROUPS + depth):
-            for name, lag in ORDER:
-                if is_group(n - lag):
-                    fns[name](n - lag)
+            order = ORDER
+            if n in O.get('mfirst', ()):
+                order = [p for p in ORDER if p[0][0] in "LMS" and p[0] != "SQ"] + [p for p in ORDER if not (p[0][0] in "LMS" and p[0] != "SQ")]
+            for name, lag in order:
+                for g in (n - lag, n - lag + 1):
+                    early = 1 if late(name) and g >= GROUPS - O.get('early', 0) else 0
+                    if is_group(g) and g + lag - early == n:
+                        fns[name](g)

@@ -28,6 +28,11 @@ CFG = dict(
     xfirst=1,
     xsplit=1,
     ag=(0, 5),
+    tail2=2,
+    lastring=1,
+    sqlast=2,
+    dtail=2,
+    a0d=1,
 )
 
 SIZES = CFG['sizes']
@@ -87,8 +92,11 @@ def tile_lintrans_pa_t_kernel(
             x_tiles[g] = x_sb
 
         def load_more(g):
-            if AHEAD <= g + AHEAD < GROUPS:
+            if AHEAD <= g + AHEAD <= GROUPS - O.get('mates', 1):
                 load_x(g + AHEAD)
+            if O.get('mates') and g + AHEAD == GROUPS - O['mates']:
+                for k in range(g + AHEAD + 1, GROUPS):
+                    load_x(k)
 
         w1s_raw = consts.tile([P, H0], U8, align_bytes=64)
         nc.vector.memset(w1s_raw[:].bitcast(I32), 0)
@@ -312,6 +320,8 @@ def tile_lintrans_pa_t_kernel(
             zt_bank[g, half] = z_t_ps
 
         def splits(g):
+            if O.get('s01') is not None and g % 2 == O['s01'] and 0 < g < GROUPS - O.get('s01tail', 0):
+                return (0, 1)
             return O['split'] if g < GROUPS - O.get('sa', 0) else ()
 
         def copy_zt(g, half, part=0):
@@ -344,7 +354,10 @@ def tile_lintrans_pa_t_kernel(
                 z_transposed[g, half] = (hi, lo)
             elif part == 0:
                 hi = work.tile([P, SIZES[g] * P], BF16, name="z_hi%d" % half)
-                nc.scalar.activation(out=hi[:], in_=z_t_ps[:], func=ACT.Identity, bias=bias, scale=1.0)
+                if half == 0 and O.get('hi0') == 'D':
+                    nc.vector.tensor_scalar_add(out=hi[:], in0=z_t_ps[:], scalar1=bias)
+                else:
+                    nc.scalar.activation(out=hi[:], in_=z_t_ps[:], func=ACT.Identity, bias=bias, scale=1.0)
                 z_transposed[g, half] = (hi,)
             else:
                 lo = work.tile([P, SIZES[g] * P], BF16, name="z_lo%d" % half)
@@ -358,7 +371,7 @@ def tile_lintrans_pa_t_kernel(
             for i in range(lo, min(hi, SIZES[g])):
                 t = FIRST[g] + i
                 squares = work.tile([P, H1], BF16)
-                if not (O.get('sqd') and g % O['sqd'] == 1 and i == SIZES[g] - 1 and 0 < g < GROUPS - 2):
+                if not (g == GROUPS - 1 and i >= SIZES[g] - O.get('sqlast', 0)) and not (O.get('sqd') and g % O['sqd'] == 1 and i == SIZES[g] - 1 and 0 < g < GROUPS - 2):
                     nc.scalar.activation(
                         out=squares[:], in_=z_tiles[g][:, i, :], func=ACT.Square, accum_out=z_norm[:, t : t + 1]
                     )
@@ -378,7 +391,7 @@ def tile_lintrans_pa_t_kernel(
             shape = [P, BATCHES[batch], K]
             if k == 0:
                 denom = work.tile(shape, F32)
-                (nc.gpsimd if 0 in O.get('ag', ()) else nc.vector).tensor_tensor(
+                (nc.gpsimd if 0 in O.get('ag', ()) and not (O.get('a0d') and batch >= len(BATCHES) - O['a0d']) else nc.vector).tensor_tensor(
                     out=denom[:],
                     in0=z_norm[:, tiles].unsqueeze(2).to_broadcast(shape),
                     in1=c_norm1[:].unsqueeze(1).to_broadcast(shape),
@@ -391,6 +404,11 @@ def tile_lintrans_pa_t_kernel(
                     out=denom2[:], in0=dist_tiles[batch][:], in1=kernels[batch, 0][:], op=ALU.add
                 )
                 kernels[batch, k] = denom2
+            if k == 2 and O.get('lastsplit') and batch == len(BATCHES) - 1:
+                lo = FIRST[GROUPS - 1] - BFIRST[batch]
+                nc.vector.tensor_tensor(
+                    out=kernels[batch, 1][:, lo:, :], in0=kernels["rest"][:], in1=kernels[batch, 1][:, lo:, :], op=ALU.add
+                )
             if k == 2:
                 kernel = work.tile(shape, F32)
                 nc.vector.reciprocal(out=kernel[:], in_=kernels[batch, 1][:])
@@ -404,7 +422,7 @@ def tile_lintrans_pa_t_kernel(
                 nc.vector.reciprocal(out=inverse[:], in_=kernels[batch, 3][:])
                 kernels[batch, k] = inverse
             if k == 5:
-                (nc.gpsimd if 5 in O.get('ag', ()) and batch < len(BATCHES) - 1 else nc.vector).tensor_tensor(
+                (nc.gpsimd if 5 in O.get('ag', ()) and batch < len(BATCHES) - O.get('dtail', 1) else nc.vector).tensor_tensor(
                     out=q_sb[:, tiles, :], in0=kernels[batch, 2][:], in1=kernels[batch, 4][:].unsqueeze(2).to_broadcast(shape), op=ALU.mult
                 )
                 nc.sync.dma_start(out=q_rows[:, tiles, :], in_=q_sb[:, tiles, :])
@@ -413,16 +431,38 @@ def tile_lintrans_pa_t_kernel(
             return 0 <= g < GROUPS
 
         def step(k):
-            return lambda g: assign(batch_of(g), k) if FIRST[g] + SIZES[g] == BFIRST[batch_of(g)] + BATCHES[batch_of(g)] else None
+            return lambda g: assign(batch_of(g), k) if batch_of(g) < len(BATCHES) - O.get('tail2', 0) and FIRST[g] + SIZES[g] == BFIRST[batch_of(g)] + BATCHES[batch_of(g)] else None
 
-        def products(g, i):
+        def products(g, i, part=None):
             batch = batch_of(g)
-            if FIRST[g] == BFIRST[batch] and i == 0:
-                dist_ps = dist_bank.tile([P, BATCHES[batch], K], F32)
+            if FIRST[g] == BFIRST[batch] and i == 0 and part != 1:
+                if batch >= len(BATCHES) - O.get('lastring', 0):
+                    dist_ps = banks.tile([P, BATCHES[batch], K], F32, tag=BT)
+                else:
+                    dist_ps = dist_bank.tile([P, BATCHES[batch], K], F32)
                 dist_tiles[batch] = dist_ps
+            if O.get('lastsplit') and g == GROUPS - 1:
+                if i == 0:
+                    rest = banks.tile([P, SIZES[g], K], F32, tag=BT)
+                    kernels["rest"] = rest
+                for half in range(2):
+                    for r in range(SIZES[g]):
+                        if (half == 0) == (i == 0) and i < 2:
+                            parts = z_transposed[g, half]
+                            for m, t in enumerate(parts):
+                                nc.tensor.matmul(
+                                    out=(dist_tiles[batch][:, FIRST[g] - BFIRST[batch] + r, :] if half == 0 else kernels["rest"][:, r, :]),
+                                    lhsT=t[:, r * P : (r + 1) * P],
+                                    rhs=(c_minus2_bf if half in splits(g) else c_minus2)[:, half, :],
+                                    start=(m == 0),
+                                    stop=(m == len(parts) - 1),
+                                )
+                return
             if i < SIZES[g]:
                 ops = [(t, half) for half in range(2) for t in z_transposed[g, half]]
                 for m, (t, half) in enumerate(ops):
+                    if part is not None and half != part:
+                        continue
                     nc.tensor.matmul(
                         out=dist_tiles[batch][:, FIRST[g] - BFIRST[batch] + i, :],
                         lhsT=t[:, i * P : (i + 1) * P],
@@ -432,6 +472,10 @@ def tile_lintrans_pa_t_kernel(
                     )
 
         fns = dict(
+            U0=lambda g: transpose_x(g + 1, 0) if g + 1 < GROUPS else None,
+            U1=lambda g: transpose_x(g + 1, 1) if g + 1 < GROUPS else None,
+            Y0=lambda g: copy_x(g + 1, 0) if g + 1 < GROUPS else None,
+            Y1=lambda g: copy_x(g + 1, 1) if g + 1 < GROUPS else None,
             L=load_more,  T0=lambda g: transpose_x(g, 0), T1=lambda g: transpose_x(g, 1), X0=lambda g: copy_x(g, 0), X1=lambda g: copy_x(g, 1),
             QX=quantise_x, RG=regroup_h, RA=lambda g: regroup_h(g, 0, 2), RB=lambda g: regroup_h(g, 1, 2), QH=quantise_h,
             Z0=lambda g: second_matmul(g, 0), Z1=lambda g: second_matmul(g, 1), A0=lambda g: add_b2(g, 0), A1=lambda g: add_b2(g, 1),
@@ -442,22 +486,44 @@ def tile_lintrans_pa_t_kernel(
         for s in range(4):
             fns["M%d" % s] = lambda g, s=s: first_matmul(g, s)
             fns["d%d" % s] = lambda g, s=s: products(g, s)
+            fns["e%d" % s] = lambda g, s=s: products(g, s, 0)
+            fns["f%d" % s] = lambda g, s=s: products(g, s, 1)
             fns["q%d" % s] = lambda g, s=s: norms(g, s, s + 1)
             fns["S%d" % s] = lambda g, s=s: silu(g, s)
         for s in range(1, 5):
             fns["k%d" % s] = lambda g, s=s: constants(s) if g == 0 else None
         for s in range(6):
             fns["a%d" % s] = step(s)
-        depth = max(lag for name, lag in ORDER)
+        depth = 6 if O.get('pair') else max(lag for name, lag in ORDER)
         def late(name):
             return name[0] in "ZAVWwSdqa" and name not in ("S0", "S1", "S2", "S3")
 
         for n in range(GROUPS + depth):
             order = ORDER
+            if O.get('pair'):
+                ev, od = O['pair']
+                order = [(w.split('-')[0], int(w.split('-')[1])) for w in (od if n % 2 else ev).split()]
             if n in O.get('mfirst', ()):
                 order = [p for p in ORDER if p[0][0] in "LMS" and p[0] != "SQ"] + [p for p in ORDER if not (p[0][0] in "LMS" and p[0] != "SQ")]
+            if O.get('mates'):
+                runs = []
+                for name, lag in order:
+                    if runs and runs[-1][0] == lag:
+                        runs[-1][1].append(name)
+                    else:
+                        runs.append((lag, [name]))
+                for lag, names in runs:
+                    for g in range(GROUPS):
+                        if min(g, GROUPS - O['mates']) + lag == n:
+                            for name in names:
+                                fns[name](g)
+                continue
             for name, lag in order:
-                for g in (n - lag, n - lag + 1):
+                for g in (n - lag,) if O.get('pair') else (n - lag, n - lag + 1):
                     early = 1 if late(name) and g >= GROUPS - O.get('early', 0) else 0
                     if is_group(g) and g + lag - early == n:
                         fns[name](g)
+        if O.get('tail2'):
+            for k in range(6):
+                for b in range(len(BATCHES) - O['tail2'], len(BATCHES)):
+                    assign(b, k)

@@ -17,32 +17,14 @@ P = 128
 PACK = 4
 ROWS, D_IN, H0, H1, K = 8192, 512, 512, 256, 20
 TILES = ROWS // P
-CFG = dict(
-    sizes=[4] * 16,
-    order="L-0 T0-0 X0-0 T1-0 X1-0 RG-2 a0-5 QX-0 k1-0 a1-5 M0-1 S0-1 M1-1 S1-1 M2-1 S2-1 M3-1 S3-1 k3-1 k4-1 QH-2 k2-0 a2-5 Z0-3 A0-3 a3-5 Z1-3 A1-3 a4-5 V0-3 W0-3 w0-3 a5-5 V1-3 W1-3 w1-3 SQ-4 d0-4 d1-4 d2-4 d3-4",
-    xc="AA",
-    zt="DA",
-    split=(1,),
-    za=3,
-    gq=1,
-    xfirst=1,
-    xsplit=1,
-    ag=(0, 5),
-    tail2=2,
-    lastring=1,
-    sqlast=2,
-    dtail=2,
-    a0d=1,
-)
-
-SIZES = CFG['sizes']
-ORDER = [(w.split('-')[0], int(w.split('-')[1])) for w in CFG['order'].split()]
-O = CFG
-GROUPS = len(SIZES)
-FIRST = [sum(SIZES[:g]) for g in range(GROUPS)]
-AHEAD = CFG.get("ahead", 4)
-BATCHES = CFG.get('batches', [8] * 8)
-BFIRST = [sum(BATCHES[:b]) for b in range(len(BATCHES))]
+GROUP = 4
+GROUPS = TILES // GROUP
+COLS = GROUP * P
+AHEAD = 4
+BATCH = 2
+BATCH_TILES = BATCH * GROUP
+BATCHES = GROUPS // BATCH
+SCALAR_TAIL = 3
 
 FLOPS = 2 * ROWS * (D_IN * H0 + H0 * H1 + H1 * K)
 
@@ -59,44 +41,23 @@ def tile_lintrans_pa_t_kernel(
         consts = ctx.enter_context(tc.tile_pool(name="consts", bufs=1))
         x_pool = ctx.enter_context(tc.tile_pool(name="x_pool", bufs=AHEAD + 2))
         work = ctx.enter_context(tc.tile_pool(name="work", bufs=3))
-        if O.get('pools'):
-            a, b, c = O['pools']
-            xbank = ctx.enter_context(tc.psum_pool(name="xbank", bufs=a))
-            hbank = ctx.enter_context(tc.psum_pool(name="hbank", bufs=b))
-            zbank = ctx.enter_context(tc.psum_pool(name="zbank", bufs=c))
-            XTAG, HTAG, ZTAG = "x", "h", "z"
-            banks = hbank
-            BT = "h"
-        else:
-            banks = ctx.enter_context(tc.psum_pool(name="banks", bufs=7))
-            xbank = hbank = zbank = banks
-            XTAG = HTAG = ZTAG = BT = "bank"
+        banks = ctx.enter_context(tc.psum_pool(name="banks", bufs=7))
         dist_bank = ctx.enter_context(tc.psum_pool(name="dist_bank", bufs=1))
         ctx.enter_context(tc.manual_schedule())
 
-        x_tiles, x_grouped, x_quantised = {}, {}, {}
-        h_rows, h_grouped, h_quantised = {}, {}, {}
-        z_tiles, z_transposed, dist_tiles = {}, {}, {}
-        x_trans, h_bank, z_bank, zt_bank = {}, {}, {}, {}
+        x_tiles, x_trans, x_quantised = {}, {}, {}
+        h_ps_tiles, h_rows, h_quantised = {}, {}, {}
+        z_ps_tiles, z_tiles, zt_ps_tiles = {}, {}, {}
+        zt_whole, zt_head, zt_rest = {}, {}, {}
+        dist_tiles, norms_tiles, kernel_tiles, denom_tiles, inverse_tiles, total_tiles = {}, {}, {}, {}, {}, {}
+        x_grouped, h_grouped = {}, {}
 
-        def tiles_of(g):
-            return slice(FIRST[g], FIRST[g] + SIZES[g])
-
-        def load_x(g):
-            x_sb = x_pool.tile([P, SIZES[g], D_IN], BF16)
-            step = 2 if g < O.get('xsplit', 0) else SIZES[g]
-            for i in range(0, SIZES[g], step):
-                nc.sync.dma_start(
-                    out=x_sb[:, i : i + step, :], in_=x_rows[:, FIRST[g] + i : FIRST[g] + i + step, :]
-                )
+        def load_x(g, pieces=1):
+            x_sb = x_pool.tile([P, GROUP, D_IN], BF16)
+            n = GROUP // pieces
+            for i in range(0, GROUP, n):
+                nc.sync.dma_start(out=x_sb[:, i : i + n, :], in_=x_rows[:, g * GROUP + i : g * GROUP + i + n, :])
             x_tiles[g] = x_sb
-
-        def load_more(g):
-            if AHEAD <= g + AHEAD <= GROUPS - O.get('mates', 1):
-                load_x(g + AHEAD)
-            if O.get('mates') and g + AHEAD == GROUPS - O['mates']:
-                for k in range(g + AHEAD + 1, GROUPS):
-                    load_x(k)
 
         w1s_raw = consts.tile([P, H0], U8, align_bytes=64)
         nc.vector.memset(w1s_raw[:].bitcast(I32), 0)
@@ -107,9 +68,8 @@ def tile_lintrans_pa_t_kernel(
         ident = consts.tile([P, P], F32)
         make_identity(nc, ident[:])
 
-        load_x(0)
-        if O.get('xfirst'):
-            load_x(1)
+        load_x(0, pieces=2)
+        load_x(1)
         w1_raw = consts.tile([P, H0], U32, align_bytes=64)
         nc.sync.dma_start(
             out=w1_raw[:].bitcast(I32),
@@ -122,10 +82,8 @@ def tile_lintrans_pa_t_kernel(
             )
         b1_bf = consts.tile([P, PACK], BF16)
         nc.gpsimd.dma_start(out=b1_bf[:], in_=b1.rearrange("(m t) -> m t", t=PACK))
-        if not O.get('xfirst'):
-            load_x(1)
-        (nc.gpsimd if O.get('gq') else nc.sync).dma_start(out=small[0:K, :, :], in_=clusters.rearrange("k (h j) -> k h j", h=2))
-        (nc.gpsimd if O.get('gq') else nc.sync).dma_start(out=small[K : K + 1, :, :], in_=b2.rearrange("(o h j) -> o h j", o=1, h=2))
+        nc.gpsimd.dma_start(out=small[0:K, :, :], in_=clusters.rearrange("k (h j) -> k h j", h=2))
+        nc.gpsimd.dma_start(out=small[K : K + 1, :, :], in_=b2.rearrange("(o h j) -> o h j", o=1, h=2))
         w2c = consts.tile([P, H1], U32, align_bytes=64)
         nc.sync.dma_start(
             out=w2c[:].bitcast(I32),
@@ -154,131 +112,115 @@ def tile_lintrans_pa_t_kernel(
         b2_cols = small_t[:, :, K]
         b2_bc = consts.tile([P, H1], F32)
         c_minus2 = consts.tile([P, 2, K], F32)
-        c_minus2_bf = consts.tile([P, 2, K], BF16)
+        c_minus2_bf = consts.tile([P, K], BF16)
         c_sq = consts.tile([P, H1], F32)
         c_len = consts.tile([P, 1], F32)
         c_diag = consts.tile([P, K], F32)
         c_norm1 = consts.tile([P, K], F32)
         ones = consts.tile([P, P], F32)
-        row = consts.tile([P, P], F32)
-
+        b2_row = consts.tile([P, P], F32)
         const_ps = {}
 
-        def constants(k):
-            if k == 1:
-                nc.gpsimd.memset(ones[:], 1.0)
-                nc.vector.tensor_copy(out=small_f[:], in_=small[:])
-                nc.vector.tensor_scalar_mul(out=row[:], in0=ones[:], scalar1=ident[:, K : K + 1])
-                flat = small_f[:].rearrange("p h j -> p (h j)")
-                nc.vector.scalar_tensor_tensor(
-                    out=c_sq[:], in0=flat, scalar=1.0, in1=flat, op0=ALU.mult, op1=ALU.mult, accum_out=c_len[:]
-                )
-            if k == 2:
-                nc.vector.tensor_scalar_mul(out=c_diag[:], in0=ident[:, 0:K], scalar1=c_len[:])
-            if k == 3:
-                small_ps = banks.tile([P, 2, P], F32, tag=BT)
-                for half in range(2):
-                    nc.tensor.transpose(out=small_ps[:, half, :], in_=small_f[:, half, :], identity=ident[:])
-                b2_ps = banks.tile([P, H1 + K], F32, tag=BT)
-                nc.tensor.matmul(out=b2_ps[:, 0:H1], lhsT=row[:], rhs=small_f[:].rearrange("p h j -> p (h j)"), start=True, stop=True)
-                nc.tensor.matmul(out=b2_ps[:, H1:], lhsT=ones[:], rhs=c_diag[:], start=True, stop=True)
-                const_ps[0] = small_ps
-                const_ps[1] = b2_ps
-            if k == 4:
-                nc.vector.tensor_copy(out=small_t[:], in_=const_ps[0][:])
-                nc.vector.tensor_copy(out=b2_bc[:], in_=const_ps[1][:, 0:H1])
-                nc.vector.tensor_scalar_add(out=c_norm1[:], in0=const_ps[1][:, H1:], scalar1=1.0)
-                nc.vector.tensor_scalar_mul(out=c_minus2[:], in0=c_t, scalar1=-2.0)
-                if O["split"]:
-                    nc.vector.tensor_scalar_mul(out=c_minus2_bf[:], in0=c_t, scalar1=-2.0)
+        def constants_rows():
+            nc.gpsimd.memset(ones[:], 1.0)
+            nc.vector.tensor_copy(out=small_f[:], in_=small[:])
+            nc.vector.tensor_scalar_mul(out=b2_row[:], in0=ones[:], scalar1=ident[:, K : K + 1])
+            flat = small_f[:].rearrange("p h j -> p (h j)")
+            nc.vector.scalar_tensor_tensor(
+                out=c_sq[:], in0=flat, scalar=1.0, in1=flat, op0=ALU.mult, op1=ALU.mult, accum_out=c_len[:]
+            )
+
+        def constants_diagonal():
+            nc.vector.tensor_scalar_mul(out=c_diag[:], in0=ident[:, 0:K], scalar1=c_len[:])
+
+        def constants_tensor():
+            small_ps = banks.tile([P, 2, P], F32, tag="bank")
+            for half in range(2):
+                nc.tensor.transpose(out=small_ps[:, half, :], in_=small_f[:, half, :], identity=ident[:])
+            spread_ps = banks.tile([P, H1 + K], F32, tag="bank")
+            nc.tensor.matmul(
+                out=spread_ps[:, 0:H1], lhsT=b2_row[:], rhs=small_f[:].rearrange("p h j -> p (h j)"), start=True, stop=True
+            )
+            nc.tensor.matmul(out=spread_ps[:, H1:], lhsT=ones[:], rhs=c_diag[:], start=True, stop=True)
+            const_ps["small"] = small_ps
+            const_ps["spread"] = spread_ps
+
+        def constants_out():
+            nc.vector.tensor_copy(out=small_t[:], in_=const_ps["small"][:])
+            nc.vector.tensor_copy(out=b2_bc[:], in_=const_ps["spread"][:, 0:H1])
+            nc.vector.tensor_scalar_add(out=c_norm1[:], in0=const_ps["spread"][:, H1:], scalar1=1.0)
+            nc.vector.tensor_scalar_mul(out=c_minus2[:], in0=c_t, scalar1=-2.0)
+            nc.vector.tensor_scalar_mul(out=c_minus2_bf[:], in0=c_t[:, 1, :], scalar1=-2.0)
 
         z_norm = consts.tile([P, TILES], F32)
         q_sb = consts.tile([P, TILES, K], F32)
 
-        def transpose_x(g, f):
-            count = min(2, SIZES[g])
-            if 2 * f >= SIZES[g]:
-                return
-            x_t = xbank.tile([P, count, 2, P], F32, tag=XTAG)
-            for i in range(count):
-                words = x_tiles[g][:, 2 * f + i, :].bitcast(F32)
-                for u in range(2):
-                    nc.tensor.transpose(out=x_t[:, i, u, :], in_=words[:, u : D_IN // 2 : 2], identity=ident[:])
-            x_trans[g, f] = x_t
+        def in_float32(g):
+            return g % 4 == 1
 
-        def copy_x(g, f):
-            if 2 * f >= SIZES[g]:
-                return
-            count = min(2, SIZES[g])
-            if f == 0:
-                grouped = work.tile([P, PACK * P * SIZES[g]], BF16, align_bytes=64, name="x_grouped")
-                x_grouped[g] = grouped
-            grouped_words = x_grouped[g][:].bitcast(F32).rearrange("p (i r u) -> p i r u", i=SIZES[g], u=2)
-            e = 'D' if g < O.get('xd', 0) else O['xc'][f]
-            src = x_trans[g, f][:].rearrange("p i u r -> p i r u")
-            if e == 'A':
-                nc.scalar.copy(out=grouped_words[:, 2 * f : 2 * f + count], in_=src)
-            else:
-                nc.vector.tensor_copy(out=grouped_words[:, 2 * f : 2 * f + count], in_=src)
+        def transpose_x(g):
+            for pair in range(2):
+                x_t = banks.tile([P, 2, 2, P], F32, tag="bank")
+                for i in range(2):
+                    words = x_tiles[g][:, 2 * pair + i, :].bitcast(F32)
+                    for u in range(2):
+                        nc.tensor.transpose(out=x_t[:, i, u, :], in_=words[:, u : D_IN // 2 : 2], identity=ident[:])
+                x_trans[g, pair] = x_t
+            grouped = work.tile([P, PACK * COLS], BF16, align_bytes=64, name="x_grouped")
+            x_grouped[g] = grouped
+            words = grouped[:].bitcast(F32).rearrange("p (i r u) -> p i r u", i=GROUP, u=2)
+            for pair in range(2):
+                nc.scalar.copy(
+                    out=words[:, 2 * pair : 2 * pair + 2], in_=x_trans[g, pair][:].rearrange("p i u r -> p i r u")
+                )
+
+        def regroup_h(g):
+            grouped = work.tile([P, PACK * COLS], BF16, align_bytes=64, name="h_grouped")
+            h_grouped[g] = grouped
+            nc.vector.tensor_copy(
+                out=grouped[:].rearrange("p (c i t) -> p c t i", i=4, t=PACK),
+                in_=h_rows[g][:].rearrange("p t (c i) -> p c t i", i=4),
+            )
 
         def quantise_x(g):
-            cols = SIZES[g] * P
-            codes = work.tile([P, cols], U32, align_bytes=64, name="x_codes")
-            scales = work.tile([P, cols], U8, align_bytes=64, name="x_scales")
+            codes = work.tile([P, COLS], U32, align_bytes=64, name="x_codes")
+            scales = work.tile([P, COLS], U8, align_bytes=64, name="x_scales")
             nc.vector.quantize_mx(out=codes[:].bitcast(FP8X4), scales=scales[:], in_=x_grouped[g][:])
-            x_quantised[g] = (codes, scales)
-
-        def first_matmul(g, s):
-            codes, scales = x_quantised[g]
-            cols = SIZES[g] * P
-            h_ps = hbank.tile([P, cols], F32, tag=HTAG)
-            nc.tensor.matmul_mx(
-                out=h_ps[:],
-                lhsT=w1c[:, s, :].bitcast(FP8X4),
-                lhsT_scale=w1s[:, s, :],
-                rhs=codes[:].bitcast(FP8X4),
-                rhs_scale=scales[:],
-                start=True,
-                stop=True,
-            )
-            h_bank[g, s] = h_ps
-
-        def silu(g, s):
-            if s == 0:
-                h_t = work.tile([P, PACK, SIZES[g] * P], BF16)
-                h_rows[g] = h_t
-            nc.scalar.activation(
-                out=h_rows[g][:, s, :], in_=h_bank[g, s][:], func=ACT.Silu, bias=b1_cols[:, s : s + 1], scale=1.0
-            )
-
-        def regroup_h(g, part=0, parts=1):
-            if part == 0:
-                grouped = work.tile([P, SIZES[g] * P, PACK], BF16, align_bytes=64, name="h_grouped")
-                h_grouped[g] = grouped
-            n = SIZES[g] * P // parts
-            cols = slice(part * n, (part + 1) * n)
-            nc.vector.tensor_copy(
-                out=h_grouped[g][:, cols, :].rearrange("p (c i) t -> p c t i", i=4),
-                in_=h_rows[g][:, :, cols].rearrange("p t (c i) -> p c t i", i=4),
-            )
+            x_quantised[g] = (codes[:], scales[:])
 
         def quantise_h(g):
-            cols = SIZES[g] * P
-            codes = work.tile([P, cols], U32, align_bytes=64, name="h_codes")
-            scales = work.tile([P, cols], U8, align_bytes=64, name="h_scales")
-            nc.vector.quantize_mx(
-                out=codes[:].bitcast(FP8X4), scales=scales[:], in_=h_grouped[g][:].rearrange("p c t -> p (c t)")
-            )
-            h_quantised[g] = (codes, scales)
+            codes = work.tile([P, COLS], U32, align_bytes=64, name="h_codes")
+            scales = work.tile([P, COLS], U8, align_bytes=64, name="h_scales")
+            nc.vector.quantize_mx(out=codes[:].bitcast(FP8X4), scales=scales[:], in_=h_grouped[g][:])
+            h_quantised[g] = (codes[:], scales[:])
 
-        def second_matmul(g, f):
-            if 2 * f >= SIZES[g]:
-                return
+        def first_matmul(g):
+            codes, scales = x_quantised[g]
+            h_t = work.tile([P, PACK, COLS], BF16)
+            for s in range(PACK):
+                h_ps = banks.tile([P, COLS], F32, tag="bank")
+                nc.tensor.matmul_mx(
+                    out=h_ps[:],
+                    lhsT=w1c[:, s, :].bitcast(FP8X4),
+                    lhsT_scale=w1s[:, s, :],
+                    rhs=codes.bitcast(FP8X4),
+                    rhs_scale=scales,
+                    start=True,
+                    stop=True,
+                )
+                nc.scalar.activation(
+                    out=h_t[:, s, :], in_=h_ps[:], func=ACT.Silu, bias=b1_cols[:, s : s + 1], scale=1.0
+                )
+            h_rows[g] = h_t
+
+        def second_matmul(g, pair):
             codes, scales = h_quantised[g]
-            count = min(2, SIZES[g])
-            z_ps = zbank.tile([P, count, H1], F32, tag=ZTAG)
-            for i in range(count):
-                cols = slice((2 * f + i) * P, (2 * f + i + 1) * P)
+            if pair == 0:
+                z_sb = work.tile([P, GROUP, H1], F32)
+                z_tiles[g] = z_sb
+            z_ps = banks.tile([P, 2, H1], F32, tag="bank")
+            for i in range(2):
+                cols = slice((2 * pair + i) * P, (2 * pair + i + 1) * P)
                 nc.tensor.matmul_mx(
                     out=z_ps[:, i, :],
                     lhsT=codes[:, cols].bitcast(FP8X4),
@@ -288,242 +230,170 @@ def tile_lintrans_pa_t_kernel(
                     start=True,
                     stop=True,
                 )
-            z_bank[g, f] = z_ps
-
-        def add_b2(g, f):
-            if f == 0:
-                z_sb = work.tile([P, SIZES[g], H1], F32)
-                z_tiles[g] = z_sb
-            count = min(2, SIZES[g])
-            if 2 * f < SIZES[g]:
-                nc.vector.tensor_tensor(
-                    out=z_tiles[g][:, 2 * f : 2 * f + count, :],
-                    in0=z_bank[g, f][:],
-                    in1=b2_bc[:].unsqueeze(1).to_broadcast([P, count, H1]),
-                    op=ALU.add,
-                )
-            if f == 1:
-                nc.sync.dma_start(out=z_rows[:, tiles_of(g), :], in_=z_tiles[g][:])
+            nc.vector.tensor_tensor(
+                out=z_tiles[g][:, 2 * pair : 2 * pair + 2, :],
+                in0=z_ps[:],
+                in1=b2_bc[:].unsqueeze(1).to_broadcast([P, 2, H1]),
+                op=ALU.add,
+            )
+            if pair == 1:
+                nc.sync.dma_start(out=z_rows[:, g * GROUP : (g + 1) * GROUP, :], in_=z_tiles[g][:])
 
         def second_transposed(g, half):
             codes, scales = h_quantised[g]
-            z_t_ps = zbank.tile([P, SIZES[g] * P], F32, tag=ZTAG)
+            zt_ps = banks.tile([P, COLS], F32, tag="bank")
             nc.tensor.matmul_mx(
-                out=z_t_ps[:],
+                out=zt_ps[:],
                 lhsT=w2c[:, half * P : (half + 1) * P].bitcast(FP8X4),
                 lhsT_scale=w2s[:, half * P : (half + 1) * P],
-                rhs=codes[:].bitcast(FP8X4),
-                rhs_scale=scales[:],
+                rhs=codes.bitcast(FP8X4),
+                rhs_scale=scales,
                 start=True,
                 stop=True,
             )
-            zt_bank[g, half] = z_t_ps
-
-        def splits(g):
-            if O.get('s01') is not None and g % 2 == O['s01'] and 0 < g < GROUPS - O.get('s01tail', 0):
-                return (0, 1)
-            return O['split'] if g < GROUPS - O.get('sa', 0) else ()
-
-        def copy_zt(g, half, part=0):
-            z_t_ps = zt_bank[g, half]
             bias = b2_cols[:, half : half + 1]
-            if half not in splits(g):
-                if part == 1:
-                    return
-                z_t = work.tile([P, SIZES[g] * P], F32, name="z_t%d" % half)
-                z_transposed[g, half] = (z_t,)
-                if O['zt'][half] == 'D' and g < GROUPS - O.get('za', 0):
-                    nc.vector.tensor_scalar_add(out=z_t[:], in0=z_t_ps[:], scalar1=bias)
+            if half == 0 or in_float32(g):
+                whole = work.tile([P, COLS], F32, name="zt_whole_%d" % half)
+                if g < GROUPS - SCALAR_TAIL:
+                    nc.vector.tensor_scalar_add(out=whole[:], in0=zt_ps[:], scalar1=bias)
                 else:
-                    nc.scalar.activation(out=z_t[:], in_=z_t_ps[:], func=ACT.Identity, bias=bias, scale=1.0)
-            elif half in O.get('gp', ()):
-                if part == 1:
-                    return
-                z_t = work.tile([P, SIZES[g] * P], F32, name="z_t%d" % half)
-                if O['zt'][half] == 'D':
-                    nc.vector.tensor_scalar_add(out=z_t[:], in0=z_t_ps[:], scalar1=bias)
-                else:
-                    nc.scalar.activation(out=z_t[:], in_=z_t_ps[:], func=ACT.Identity, bias=bias, scale=1.0)
-                hi = work.tile([P, SIZES[g] * P], BF16, name="z_hi%d" % half)
-                lo = work.tile([P, SIZES[g] * P], BF16, name="z_lo%d" % half)
-                n = min(O.get('gcols', 512), SIZES[g] * P)
-                for c0 in range(0, SIZES[g] * P, n):
-                    cs = slice(c0, c0 + n)
-                    nc.gpsimd.tensor_scalar(out=hi[:, cs], in0=z_t[:, cs], scalar1=1.0, scalar2=0.0, op0=ALU.mult, op1=ALU.add)
-                    nc.gpsimd.tensor_tensor(out=lo[:, cs], in0=z_t[:, cs], in1=hi[:, cs], op=ALU.subtract)
-                z_transposed[g, half] = (hi, lo)
-            elif part == 0:
-                hi = work.tile([P, SIZES[g] * P], BF16, name="z_hi%d" % half)
-                if half == 0 and O.get('hi0') == 'D':
-                    nc.vector.tensor_scalar_add(out=hi[:], in0=z_t_ps[:], scalar1=bias)
-                else:
-                    nc.scalar.activation(out=hi[:], in_=z_t_ps[:], func=ACT.Identity, bias=bias, scale=1.0)
-                z_transposed[g, half] = (hi,)
+                    nc.scalar.activation(out=whole[:], in_=zt_ps[:], func=ACT.Identity, bias=bias, scale=1.0)
+                zt_whole[g, half] = whole
             else:
-                lo = work.tile([P, SIZES[g] * P], BF16, name="z_lo%d" % half)
-                hi = z_transposed[g, half][0]
-                nc.vector.scalar_tensor_tensor(
-                    out=lo[:], in0=z_t_ps[:], scalar=bias, in1=hi[:], op0=ALU.add, op1=ALU.subtract
-                )
-                z_transposed[g, half] = (hi, lo)
+                head = work.tile([P, COLS], BF16)
+                nc.scalar.activation(out=head[:], in_=zt_ps[:], func=ACT.Identity, bias=bias, scale=1.0)
+                zt_head[g] = head
+                zt_ps_tiles[g] = zt_ps
 
-        def norms(g, lo=0, hi=4):
-            for i in range(lo, min(hi, SIZES[g])):
-                t = FIRST[g] + i
+        def remainder(g):
+            if in_float32(g):
+                return
+            rest = work.tile([P, COLS], BF16)
+            nc.vector.scalar_tensor_tensor(
+                out=rest[:],
+                in0=zt_ps_tiles[g][:],
+                scalar=b2_cols[:, 1:2],
+                in1=zt_head[g][:],
+                op0=ALU.add,
+                op1=ALU.subtract,
+            )
+            zt_rest[g] = rest
+
+        def norms(g):
+            for i in range(GROUP):
+                t = g * GROUP + i
+                row = z_tiles[g][:, i, :]
                 squares = work.tile([P, H1], BF16)
-                if not (g == GROUPS - 1 and i >= SIZES[g] - O.get('sqlast', 0)) and not (O.get('sqd') and g % O['sqd'] == 1 and i == SIZES[g] - 1 and 0 < g < GROUPS - 2):
-                    nc.scalar.activation(
-                        out=squares[:], in_=z_tiles[g][:, i, :], func=ACT.Square, accum_out=z_norm[:, t : t + 1]
-                    )
+                if g < GROUPS - 1 or i < GROUP // 2:
+                    nc.scalar.activation(out=squares[:], in_=row, func=ACT.Square, accum_out=z_norm[:, t : t + 1])
                 else:
                     nc.vector.scalar_tensor_tensor(
-                        out=squares[:], in0=z_tiles[g][:, i, :], scalar=1.0, in1=z_tiles[g][:, i, :], op0=ALU.mult, op1=ALU.mult,
-                        accum_out=z_norm[:, t : t + 1]
+                        out=squares[:],
+                        in0=row,
+                        scalar=1.0,
+                        in1=row,
+                        op0=ALU.mult,
+                        op1=ALU.mult,
+                        accum_out=z_norm[:, t : t + 1],
                     )
 
-        kernels = {}
+        def distances(g):
+            if g % BATCH == 0:
+                if g // BATCH < BATCHES - 1:
+                    dist_ps = dist_bank.tile([P, BATCH_TILES, K], F32)
+                else:
+                    dist_ps = banks.tile([P, BATCH_TILES, K], F32, tag="bank")
+                dist_tiles[g // BATCH] = dist_ps
+            for i in range(GROUP):
+                cols = slice(i * P, (i + 1) * P)
+                if in_float32(g):
+                    factors = [(zt_whole[g, 0], c_minus2[:, 0, :]), (zt_whole[g, 1], c_minus2[:, 1, :])]
+                else:
+                    factors = [(zt_whole[g, 0], c_minus2[:, 0, :]), (zt_head[g], c_minus2_bf[:]), (zt_rest[g], c_minus2_bf[:])]
+                for m, (z_part, c_part) in enumerate(factors):
+                    nc.tensor.matmul(
+                        out=dist_tiles[g // BATCH][:, (g % BATCH) * GROUP + i, :],
+                        lhsT=z_part[:, cols],
+                        rhs=c_part,
+                        start=(m == 0),
+                        stop=(m == len(factors) - 1),
+                    )
 
-        def batch_of(g):
-            return max(b for b in range(len(BATCHES)) if BFIRST[b] <= FIRST[g])
-
-        def assign(batch, k):
-            tiles = slice(BFIRST[batch], BFIRST[batch] + BATCHES[batch])
-            shape = [P, BATCHES[batch], K]
-            if k == 0:
-                denom = work.tile(shape, F32)
-                (nc.gpsimd if 0 in O.get('ag', ()) and not (O.get('a0d') and batch >= len(BATCHES) - O['a0d']) else nc.vector).tensor_tensor(
-                    out=denom[:],
+        def assign(b, step):
+            tiles = slice(b * BATCH_TILES, (b + 1) * BATCH_TILES)
+            shape = [P, BATCH_TILES, K]
+            if step == 0:
+                norm_sum = work.tile(shape, F32)
+                engine = nc.gpsimd if b < BATCHES - 1 else nc.vector
+                engine.tensor_tensor(
+                    out=norm_sum[:],
                     in0=z_norm[:, tiles].unsqueeze(2).to_broadcast(shape),
                     in1=c_norm1[:].unsqueeze(1).to_broadcast(shape),
                     op=ALU.add,
                 )
-                kernels[batch, k] = denom
-            if k == 1:
-                denom2 = work.tile(shape, F32)
-                nc.vector.tensor_tensor(
-                    out=denom2[:], in0=dist_tiles[batch][:], in1=kernels[batch, 0][:], op=ALU.add
-                )
-                kernels[batch, k] = denom2
-            if k == 2 and O.get('lastsplit') and batch == len(BATCHES) - 1:
-                lo = FIRST[GROUPS - 1] - BFIRST[batch]
-                nc.vector.tensor_tensor(
-                    out=kernels[batch, 1][:, lo:, :], in0=kernels["rest"][:], in1=kernels[batch, 1][:, lo:, :], op=ALU.add
-                )
-            if k == 2:
+                norms_tiles[b] = norm_sum
+            elif step == 1:
+                denom = work.tile(shape, F32)
+                nc.vector.tensor_tensor(out=denom[:], in0=dist_tiles[b][:], in1=norms_tiles[b][:], op=ALU.add)
+                denom_tiles[b] = denom
+            elif step == 2:
                 kernel = work.tile(shape, F32)
-                nc.vector.reciprocal(out=kernel[:], in_=kernels[batch, 1][:])
-                kernels[batch, k] = kernel
-            if k == 3:
-                total = work.tile([P, BATCHES[batch]], F32)
-                nc.vector.tensor_reduce(out=total[:], in_=kernels[batch, 2][:], axis=AXIS.X, op=ALU.add)
-                kernels[batch, k] = total
-            if k == 4:
-                inverse = work.tile([P, BATCHES[batch]], F32)
-                nc.vector.reciprocal(out=inverse[:], in_=kernels[batch, 3][:])
-                kernels[batch, k] = inverse
-            if k == 5:
-                (nc.gpsimd if 5 in O.get('ag', ()) and batch < len(BATCHES) - O.get('dtail', 1) else nc.vector).tensor_tensor(
-                    out=q_sb[:, tiles, :], in0=kernels[batch, 2][:], in1=kernels[batch, 4][:].unsqueeze(2).to_broadcast(shape), op=ALU.mult
+                nc.vector.reciprocal(out=kernel[:], in_=denom_tiles[b][:])
+                kernel_tiles[b] = kernel
+            elif step == 3:
+                total = work.tile([P, BATCH_TILES], F32)
+                nc.vector.tensor_reduce(out=total[:], in_=kernel_tiles[b][:], axis=AXIS.X, op=ALU.add)
+                total_tiles[b] = total
+            elif step == 4:
+                inverse = work.tile([P, BATCH_TILES], F32)
+                nc.vector.reciprocal(out=inverse[:], in_=total_tiles[b][:])
+                inverse_tiles[b] = inverse
+            else:
+                engine = nc.gpsimd if b < BATCHES - 2 else nc.vector
+                engine.tensor_tensor(
+                    out=q_sb[:, tiles, :],
+                    in0=kernel_tiles[b][:],
+                    in1=inverse_tiles[b][:].unsqueeze(2).to_broadcast(shape),
+                    op=ALU.mult,
                 )
                 nc.sync.dma_start(out=q_rows[:, tiles, :], in_=q_sb[:, tiles, :])
 
-        def is_group(g):
-            return 0 <= g < GROUPS
+        def when(g, stage, *more):
+            if 0 <= g < GROUPS:
+                stage(g, *more)
 
-        def step(k):
-            return lambda g: assign(batch_of(g), k) if batch_of(g) < len(BATCHES) - O.get('tail2', 0) and FIRST[g] + SIZES[g] == BFIRST[batch_of(g)] + BATCHES[batch_of(g)] else None
+        def step_of(g, step):
+            if 0 <= g < GROUPS - 2 * BATCH and g % BATCH == BATCH - 1:
+                assign(g // BATCH, step)
 
-        def products(g, i, part=None):
-            batch = batch_of(g)
-            if FIRST[g] == BFIRST[batch] and i == 0 and part != 1:
-                if batch >= len(BATCHES) - O.get('lastring', 0):
-                    dist_ps = banks.tile([P, BATCHES[batch], K], F32, tag=BT)
-                else:
-                    dist_ps = dist_bank.tile([P, BATCHES[batch], K], F32)
-                dist_tiles[batch] = dist_ps
-            if O.get('lastsplit') and g == GROUPS - 1:
-                if i == 0:
-                    rest = banks.tile([P, SIZES[g], K], F32, tag=BT)
-                    kernels["rest"] = rest
-                for half in range(2):
-                    for r in range(SIZES[g]):
-                        if (half == 0) == (i == 0) and i < 2:
-                            parts = z_transposed[g, half]
-                            for m, t in enumerate(parts):
-                                nc.tensor.matmul(
-                                    out=(dist_tiles[batch][:, FIRST[g] - BFIRST[batch] + r, :] if half == 0 else kernels["rest"][:, r, :]),
-                                    lhsT=t[:, r * P : (r + 1) * P],
-                                    rhs=(c_minus2_bf if half in splits(g) else c_minus2)[:, half, :],
-                                    start=(m == 0),
-                                    stop=(m == len(parts) - 1),
-                                )
-                return
-            if i < SIZES[g]:
-                ops = [(t, half) for half in range(2) for t in z_transposed[g, half]]
-                for m, (t, half) in enumerate(ops):
-                    if part is not None and half != part:
-                        continue
-                    nc.tensor.matmul(
-                        out=dist_tiles[batch][:, FIRST[g] - BFIRST[batch] + i, :],
-                        lhsT=t[:, i * P : (i + 1) * P],
-                        rhs=(c_minus2_bf if half in splits(g) else c_minus2)[:, half, :],
-                        start=(m == 0),
-                        stop=(m == len(ops) - 1),
-                    )
-
-        fns = dict(
-            U0=lambda g: transpose_x(g + 1, 0) if g + 1 < GROUPS else None,
-            U1=lambda g: transpose_x(g + 1, 1) if g + 1 < GROUPS else None,
-            Y0=lambda g: copy_x(g + 1, 0) if g + 1 < GROUPS else None,
-            Y1=lambda g: copy_x(g + 1, 1) if g + 1 < GROUPS else None,
-            L=load_more,  T0=lambda g: transpose_x(g, 0), T1=lambda g: transpose_x(g, 1), X0=lambda g: copy_x(g, 0), X1=lambda g: copy_x(g, 1),
-            QX=quantise_x, RG=regroup_h, RA=lambda g: regroup_h(g, 0, 2), RB=lambda g: regroup_h(g, 1, 2), QH=quantise_h,
-            Z0=lambda g: second_matmul(g, 0), Z1=lambda g: second_matmul(g, 1), A0=lambda g: add_b2(g, 0), A1=lambda g: add_b2(g, 1),
-            V0=lambda g: second_transposed(g, 0), V1=lambda g: second_transposed(g, 1),
-            W0=lambda g: copy_zt(g, 0), W1=lambda g: copy_zt(g, 1), w0=lambda g: copy_zt(g, 0, 1), w1=lambda g: copy_zt(g, 1, 1),
-            SQ=norms, SA=lambda g: norms(g, 0, 2), SB=lambda g: norms(g, 2, 4), SQ0=lambda g: norms(g, 0, 1),
-        )
-        for s in range(4):
-            fns["M%d" % s] = lambda g, s=s: first_matmul(g, s)
-            fns["d%d" % s] = lambda g, s=s: products(g, s)
-            fns["e%d" % s] = lambda g, s=s: products(g, s, 0)
-            fns["f%d" % s] = lambda g, s=s: products(g, s, 1)
-            fns["q%d" % s] = lambda g, s=s: norms(g, s, s + 1)
-            fns["S%d" % s] = lambda g, s=s: silu(g, s)
-        for s in range(1, 5):
-            fns["k%d" % s] = lambda g, s=s: constants(s) if g == 0 else None
-        for s in range(6):
-            fns["a%d" % s] = step(s)
-        depth = 6 if O.get('pair') else max(lag for name, lag in ORDER)
-        def late(name):
-            return name[0] in "ZAVWwSdqa" and name not in ("S0", "S1", "S2", "S3")
-
-        for n in range(GROUPS + depth):
-            order = ORDER
-            if O.get('pair'):
-                ev, od = O['pair']
-                order = [(w.split('-')[0], int(w.split('-')[1])) for w in (od if n % 2 else ev).split()]
-            if n in O.get('mfirst', ()):
-                order = [p for p in ORDER if p[0][0] in "LMS" and p[0] != "SQ"] + [p for p in ORDER if not (p[0][0] in "LMS" and p[0] != "SQ")]
-            if O.get('mates'):
-                runs = []
-                for name, lag in order:
-                    if runs and runs[-1][0] == lag:
-                        runs[-1][1].append(name)
-                    else:
-                        runs.append((lag, [name]))
-                for lag, names in runs:
-                    for g in range(GROUPS):
-                        if min(g, GROUPS - O['mates']) + lag == n:
-                            for name in names:
-                                fns[name](g)
-                continue
-            for name, lag in order:
-                for g in (n - lag,) if O.get('pair') else (n - lag, n - lag + 1):
-                    early = 1 if late(name) and g >= GROUPS - O.get('early', 0) else 0
-                    if is_group(g) and g + lag - early == n:
-                        fns[name](g)
-        if O.get('tail2'):
-            for k in range(6):
-                for b in range(len(BATCHES) - O['tail2'], len(BATCHES)):
-                    assign(b, k)
+        for n in range(GROUPS + 5):
+            if n + AHEAD < GROUPS:
+                load_x(n + AHEAD)
+            when(n, transpose_x)
+            when(n - 2, regroup_h)
+            step_of(n - 5, 0)
+            when(n, quantise_x)
+            if n == 0:
+                constants_rows()
+            step_of(n - 5, 1)
+            when(n - 1, first_matmul)
+            if n == 1:
+                constants_tensor()
+                constants_out()
+            when(n - 2, quantise_h)
+            if n == 0:
+                constants_diagonal()
+            step_of(n - 5, 2)
+            when(n - 3, second_matmul, 0)
+            step_of(n - 5, 3)
+            when(n - 3, second_matmul, 1)
+            step_of(n - 5, 4)
+            when(n - 3, second_transposed, 0)
+            step_of(n - 5, 5)
+            when(n - 3, second_transposed, 1)
+            when(n - 3, remainder)
+            when(n - 4, norms)
+            when(n - 4, distances)
+        for step in range(6):
+            for b in range(BATCHES - 2, BATCHES):
+                assign(b, step)

from contextlib import ExitStack

import concourse.mybir as mybir
from concourse.masks import make_identity

F32 = mybir.dt.float32
BF16 = mybir.dt.bfloat16
I32 = mybir.dt.int32
U32 = mybir.dt.uint32
U8 = mybir.dt.uint8
FP8X4 = mybir.dt.float8_e4m3fn_x4
ACT = mybir.ActivationFunctionType
ALU = mybir.AluOpType
AXIS = mybir.AxisListType

P = 128
PACK = 4
ROWS, D_IN, H0, H1, K = 8192, 512, 512, 256, 20
TILES = ROWS // P
GROUP = 4
GROUPS = TILES // GROUP
COLS = GROUP * P
AHEAD = 4
BATCH = 2
BATCH_TILES = BATCH * GROUP
BATCHES = GROUPS // BATCH
SCALAR_TAIL = 3

FLOPS = 2 * ROWS * (D_IN * H0 + H0 * H1 + H1 * K)


def tile_lintrans_pa_t_kernel(
    tc, x, W1_words, W1_scales, b1, W2_words, W2_scales, b2, clusters, out_0, out_1
):
    nc = tc.nc
    x_rows = x.rearrange("(p t) k -> p t k", t=TILES)
    z_rows = out_0.rearrange("(p t) j -> p t j", t=TILES)
    q_rows = out_1.rearrange("(p t) k -> p t k", t=TILES)

    with ExitStack() as ctx:
        consts = ctx.enter_context(tc.tile_pool(name="consts", bufs=1))
        x_pool = ctx.enter_context(tc.tile_pool(name="x_pool", bufs=AHEAD + 2))
        work = ctx.enter_context(tc.tile_pool(name="work", bufs=3))
        banks = ctx.enter_context(tc.psum_pool(name="banks", bufs=7))
        dist_bank = ctx.enter_context(tc.psum_pool(name="dist_bank", bufs=1))
        ctx.enter_context(tc.manual_schedule())

        x_tiles, x_trans, x_quantised = {}, {}, {}
        h_ps_tiles, h_rows, h_quantised = {}, {}, {}
        z_ps_tiles, z_tiles, zt_ps_tiles = {}, {}, {}
        zt_whole, zt_head, zt_rest = {}, {}, {}
        dist_tiles, norms_tiles, kernel_tiles, denom_tiles, inverse_tiles, total_tiles = {}, {}, {}, {}, {}, {}
        x_grouped, h_grouped = {}, {}

        def load_x(g, pieces=1):
            x_sb = x_pool.tile([P, GROUP, D_IN], BF16)
            n = GROUP // pieces
            for i in range(0, GROUP, n):
                nc.sync.dma_start(out=x_sb[:, i : i + n, :], in_=x_rows[:, g * GROUP + i : g * GROUP + i + n, :])
            x_tiles[g] = x_sb

        w1s_raw = consts.tile([P, H0], U8, align_bytes=64)
        nc.vector.memset(w1s_raw[:].bitcast(I32), 0)
        small = consts.tile([P, 2, P], BF16)
        nc.vector.memset(small[:], 0.0)
        w2s = consts.tile([P, H1], U8, align_bytes=64)
        nc.vector.memset(w2s[:].bitcast(I32), 0)
        ident = consts.tile([P, P], F32)
        make_identity(nc, ident[:])

        load_x(0, pieces=2)
        load_x(1)
        w1_raw = consts.tile([P, H0], U32, align_bytes=64)
        nc.sync.dma_start(
            out=w1_raw[:].bitcast(I32),
            in_=W1_words[0].rearrange("p n t -> p (n t)").bitcast(I32),
        )
        for quad in range(4):
            nc.sync.dma_start(
                out=w1s_raw[32 * quad : 32 * quad + 4, :].bitcast(I32),
                in_=W1_scales[0, 4 * quad : 4 * quad + 4, :].bitcast(I32),
            )
        b1_bf = consts.tile([P, PACK], BF16)
        nc.gpsimd.dma_start(out=b1_bf[:], in_=b1.rearrange("(m t) -> m t", t=PACK))
        nc.gpsimd.dma_start(out=small[0:K, :, :], in_=clusters.rearrange("k (h j) -> k h j", h=2))
        nc.gpsimd.dma_start(out=small[K : K + 1, :, :], in_=b2.rearrange("(o h j) -> o h j", o=1, h=2))
        w2c = consts.tile([P, H1], U32, align_bytes=64)
        nc.sync.dma_start(
            out=w2c[:].bitcast(I32),
            in_=W2_words[0].rearrange("p n t -> p (n t)").bitcast(I32),
        )
        for quad in range(4):
            nc.sync.dma_start(
                out=w2s[32 * quad : 32 * quad + 4, :].bitcast(I32),
                in_=W2_scales[0, 4 * quad : 4 * quad + 4, :].bitcast(I32),
            )
        for g in range(2, AHEAD):
            load_x(g)

        w1c = consts.tile([P, PACK, P], U32, align_bytes=64)
        nc.vector.tensor_copy(
            out=w1c[:].bitcast(I32), in_=w1_raw[:].bitcast(I32).rearrange("p (m t) -> p t m", t=PACK)
        )
        w1s = consts.tile([P, PACK, P], U8, align_bytes=64)
        nc.vector.tensor_copy(out=w1s[:], in_=w1s_raw[:].rearrange("p (m t) -> p t m", t=PACK))
        b1_cols = consts.tile([P, PACK], F32)
        nc.vector.tensor_copy(out=b1_cols[:], in_=b1_bf[:])

        small_f = consts.tile([P, 2, P], F32)
        small_t = consts.tile([P, 2, P], F32)
        c_t = small_t[:, :, 0:K]
        b2_cols = small_t[:, :, K]
        b2_bc = consts.tile([P, H1], F32)
        c_minus2 = consts.tile([P, 2, K], F32)
        c_minus2_bf = consts.tile([P, K], BF16)
        c_sq = consts.tile([P, H1], F32)
        c_len = consts.tile([P, 1], F32)
        c_diag = consts.tile([P, K], F32)
        c_norm1 = consts.tile([P, K], F32)
        ones = consts.tile([P, P], F32)
        b2_row = consts.tile([P, P], F32)
        const_ps = {}

        def constants_rows():
            nc.gpsimd.memset(ones[:], 1.0)
            nc.vector.tensor_copy(out=small_f[:], in_=small[:])
            nc.vector.tensor_scalar_mul(out=b2_row[:], in0=ones[:], scalar1=ident[:, K : K + 1])
            flat = small_f[:].rearrange("p h j -> p (h j)")
            nc.vector.scalar_tensor_tensor(
                out=c_sq[:], in0=flat, scalar=1.0, in1=flat, op0=ALU.mult, op1=ALU.mult, accum_out=c_len[:]
            )

        def constants_diagonal():
            nc.vector.tensor_scalar_mul(out=c_diag[:], in0=ident[:, 0:K], scalar1=c_len[:])

        def constants_tensor():
            small_ps = banks.tile([P, 2, P], F32, tag="bank")
            for half in range(2):
                nc.tensor.transpose(out=small_ps[:, half, :], in_=small_f[:, half, :], identity=ident[:])
            spread_ps = banks.tile([P, H1 + K], F32, tag="bank")
            nc.tensor.matmul(
                out=spread_ps[:, 0:H1], lhsT=b2_row[:], rhs=small_f[:].rearrange("p h j -> p (h j)"), start=True, stop=True
            )
            nc.tensor.matmul(out=spread_ps[:, H1:], lhsT=ones[:], rhs=c_diag[:], start=True, stop=True)
            const_ps["small"] = small_ps
            const_ps["spread"] = spread_ps

        def constants_out():
            nc.vector.tensor_copy(out=small_t[:], in_=const_ps["small"][:])
            nc.vector.tensor_copy(out=b2_bc[:], in_=const_ps["spread"][:, 0:H1])
            nc.vector.tensor_scalar_add(out=c_norm1[:], in0=const_ps["spread"][:, H1:], scalar1=1.0)
            nc.vector.tensor_scalar_mul(out=c_minus2[:], in0=c_t, scalar1=-2.0)
            nc.vector.tensor_scalar_mul(out=c_minus2_bf[:], in0=c_t[:, 1, :], scalar1=-2.0)

        z_norm = consts.tile([P, TILES], F32)
        q_sb = consts.tile([P, TILES, K], F32)

        def in_float32(g):
            return g % 4 == 1

        def transpose_x(g):
            for pair in range(2):
                x_t = banks.tile([P, 2, 2, P], F32, tag="bank")
                for i in range(2):
                    words = x_tiles[g][:, 2 * pair + i, :].bitcast(F32)
                    for u in range(2):
                        nc.tensor.transpose(out=x_t[:, i, u, :], in_=words[:, u : D_IN // 2 : 2], identity=ident[:])
                x_trans[g, pair] = x_t
            grouped = work.tile([P, PACK * COLS], BF16, align_bytes=64, name="x_grouped")
            x_grouped[g] = grouped
            words = grouped[:].bitcast(F32).rearrange("p (i r u) -> p i r u", i=GROUP, u=2)
            for pair in range(2):
                nc.scalar.copy(
                    out=words[:, 2 * pair : 2 * pair + 2], in_=x_trans[g, pair][:].rearrange("p i u r -> p i r u")
                )

        def regroup_h(g):
            grouped = work.tile([P, PACK * COLS], BF16, align_bytes=64, name="h_grouped")
            h_grouped[g] = grouped
            nc.vector.tensor_copy(
                out=grouped[:].rearrange("p (c i t) -> p c t i", i=4, t=PACK),
                in_=h_rows[g][:].rearrange("p t (c i) -> p c t i", i=4),
            )

        def quantise_x(g):
            codes = work.tile([P, COLS], U32, align_bytes=64, name="x_codes")
            scales = work.tile([P, COLS], U8, align_bytes=64, name="x_scales")
            nc.vector.quantize_mx(out=codes[:].bitcast(FP8X4), scales=scales[:], in_=x_grouped[g][:])
            x_quantised[g] = (codes[:], scales[:])

        def quantise_h(g):
            codes = work.tile([P, COLS], U32, align_bytes=64, name="h_codes")
            scales = work.tile([P, COLS], U8, align_bytes=64, name="h_scales")
            nc.vector.quantize_mx(out=codes[:].bitcast(FP8X4), scales=scales[:], in_=h_grouped[g][:])
            h_quantised[g] = (codes[:], scales[:])

        def first_matmul(g):
            codes, scales = x_quantised[g]
            h_t = work.tile([P, PACK, COLS], BF16)
            for s in range(PACK):
                h_ps = banks.tile([P, COLS], F32, tag="bank")
                nc.tensor.matmul_mx(
                    out=h_ps[:],
                    lhsT=w1c[:, s, :].bitcast(FP8X4),
                    lhsT_scale=w1s[:, s, :],
                    rhs=codes.bitcast(FP8X4),
                    rhs_scale=scales,
                    start=True,
                    stop=True,
                )
                nc.scalar.activation(
                    out=h_t[:, s, :], in_=h_ps[:], func=ACT.Silu, bias=b1_cols[:, s : s + 1], scale=1.0
                )
            h_rows[g] = h_t

        def second_matmul(g, pair):
            codes, scales = h_quantised[g]
            if pair == 0:
                z_sb = work.tile([P, GROUP, H1], F32)
                z_tiles[g] = z_sb
            z_ps = banks.tile([P, 2, H1], F32, tag="bank")
            for i in range(2):
                cols = slice((2 * pair + i) * P, (2 * pair + i + 1) * P)
                nc.tensor.matmul_mx(
                    out=z_ps[:, i, :],
                    lhsT=codes[:, cols].bitcast(FP8X4),
                    lhsT_scale=scales[:, cols],
                    rhs=w2c[:].bitcast(FP8X4),
                    rhs_scale=w2s[:],
                    start=True,
                    stop=True,
                )
            nc.vector.tensor_tensor(
                out=z_tiles[g][:, 2 * pair : 2 * pair + 2, :],
                in0=z_ps[:],
                in1=b2_bc[:].unsqueeze(1).to_broadcast([P, 2, H1]),
                op=ALU.add,
            )
            if pair == 1:
                nc.sync.dma_start(out=z_rows[:, g * GROUP : (g + 1) * GROUP, :], in_=z_tiles[g][:])

        def second_transposed(g, half):
            codes, scales = h_quantised[g]
            zt_ps = banks.tile([P, COLS], F32, tag="bank")
            nc.tensor.matmul_mx(
                out=zt_ps[:],
                lhsT=w2c[:, half * P : (half + 1) * P].bitcast(FP8X4),
                lhsT_scale=w2s[:, half * P : (half + 1) * P],
                rhs=codes.bitcast(FP8X4),
                rhs_scale=scales,
                start=True,
                stop=True,
            )
            bias = b2_cols[:, half : half + 1]
            if half == 0 or in_float32(g):
                whole = work.tile([P, COLS], F32, name="zt_whole_%d" % half)
                if g < GROUPS - SCALAR_TAIL:
                    nc.vector.tensor_scalar_add(out=whole[:], in0=zt_ps[:], scalar1=bias)
                else:
                    nc.scalar.activation(out=whole[:], in_=zt_ps[:], func=ACT.Identity, bias=bias, scale=1.0)
                zt_whole[g, half] = whole
            else:
                head = work.tile([P, COLS], BF16)
                nc.scalar.activation(out=head[:], in_=zt_ps[:], func=ACT.Identity, bias=bias, scale=1.0)
                zt_head[g] = head
                zt_ps_tiles[g] = zt_ps

        def remainder(g):
            if in_float32(g):
                return
            rest = work.tile([P, COLS], BF16)
            nc.vector.scalar_tensor_tensor(
                out=rest[:],
                in0=zt_ps_tiles[g][:],
                scalar=b2_cols[:, 1:2],
                in1=zt_head[g][:],
                op0=ALU.add,
                op1=ALU.subtract,
            )
            zt_rest[g] = rest

        def norms(g):
            for i in range(GROUP):
                t = g * GROUP + i
                row = z_tiles[g][:, i, :]
                squares = work.tile([P, H1], BF16)
                if g < GROUPS - 1 or i < GROUP // 2:
                    nc.scalar.activation(out=squares[:], in_=row, func=ACT.Square, accum_out=z_norm[:, t : t + 1])
                else:
                    nc.vector.scalar_tensor_tensor(
                        out=squares[:],
                        in0=row,
                        scalar=1.0,
                        in1=row,
                        op0=ALU.mult,
                        op1=ALU.mult,
                        accum_out=z_norm[:, t : t + 1],
                    )

        def distances(g):
            if g % BATCH == 0:
                if g // BATCH < BATCHES - 1:
                    dist_ps = dist_bank.tile([P, BATCH_TILES, K], F32)
                else:
                    dist_ps = banks.tile([P, BATCH_TILES, K], F32, tag="bank")
                dist_tiles[g // BATCH] = dist_ps
            for i in range(GROUP):
                cols = slice(i * P, (i + 1) * P)
                if in_float32(g):
                    factors = [(zt_whole[g, 0], c_minus2[:, 0, :]), (zt_whole[g, 1], c_minus2[:, 1, :])]
                else:
                    factors = [(zt_whole[g, 0], c_minus2[:, 0, :]), (zt_head[g], c_minus2_bf[:]), (zt_rest[g], c_minus2_bf[:])]
                for m, (z_part, c_part) in enumerate(factors):
                    nc.tensor.matmul(
                        out=dist_tiles[g // BATCH][:, (g % BATCH) * GROUP + i, :],
                        lhsT=z_part[:, cols],
                        rhs=c_part,
                        start=(m == 0),
                        stop=(m == len(factors) - 1),
                    )

        def assign(b, step):
            tiles = slice(b * BATCH_TILES, (b + 1) * BATCH_TILES)
            shape = [P, BATCH_TILES, K]
            if step == 0:
                norm_sum = work.tile(shape, F32)
                engine = nc.gpsimd if b < BATCHES - 1 else nc.vector
                engine.tensor_tensor(
                    out=norm_sum[:],
                    in0=z_norm[:, tiles].unsqueeze(2).to_broadcast(shape),
                    in1=c_norm1[:].unsqueeze(1).to_broadcast(shape),
                    op=ALU.add,
                )
                norms_tiles[b] = norm_sum
            elif step == 1:
                denom = work.tile(shape, F32)
                nc.vector.tensor_tensor(out=denom[:], in0=dist_tiles[b][:], in1=norms_tiles[b][:], op=ALU.add)
                denom_tiles[b] = denom
            elif step == 2:
                kernel = work.tile(shape, F32)
                nc.vector.reciprocal(out=kernel[:], in_=denom_tiles[b][:])
                kernel_tiles[b] = kernel
            elif step == 3:
                total = work.tile([P, BATCH_TILES], F32)
                nc.vector.tensor_reduce(out=total[:], in_=kernel_tiles[b][:], axis=AXIS.X, op=ALU.add)
                total_tiles[b] = total
            elif step == 4:
                inverse = work.tile([P, BATCH_TILES], F32)
                nc.vector.reciprocal(out=inverse[:], in_=total_tiles[b][:])
                inverse_tiles[b] = inverse
            else:
                engine = nc.gpsimd if b < BATCHES - 2 else nc.vector
                engine.tensor_tensor(
                    out=q_sb[:, tiles, :],
                    in0=kernel_tiles[b][:],
                    in1=inverse_tiles[b][:].unsqueeze(2).to_broadcast(shape),
                    op=ALU.mult,
                )
                nc.sync.dma_start(out=q_rows[:, tiles, :], in_=q_sb[:, tiles, :])

        def when(g, stage, *more):
            if 0 <= g < GROUPS:
                stage(g, *more)

        def step_of(g, step):
            if 0 <= g < GROUPS - 2 * BATCH and g % BATCH == BATCH - 1:
                assign(g // BATCH, step)

        for n in range(GROUPS + 5):
            if n + AHEAD < GROUPS:
                load_x(n + AHEAD)
            when(n, transpose_x)
            when(n - 2, regroup_h)
            step_of(n - 5, 0)
            when(n, quantise_x)
            if n == 0:
                constants_rows()
            step_of(n - 5, 1)
            when(n - 1, first_matmul)
            if n == 1:
                constants_tensor()
                constants_out()
            when(n - 2, quantise_h)
            if n == 0:
                constants_diagonal()
            step_of(n - 5, 2)
            when(n - 3, second_matmul, 0)
            step_of(n - 5, 3)
            when(n - 3, second_matmul, 1)
            step_of(n - 5, 4)
            when(n - 3, second_transposed, 0)
            step_of(n - 5, 5)
            when(n - 3, second_transposed, 1)
            when(n - 3, remainder)
            when(n - 4, norms)
            when(n - 4, distances)
        for step in range(6):
            for b in range(BATCHES - 2, BATCHES):
                assign(b, step)
